import numpy as np
import ml_dtypes


def mxq(x, axis, fmt="e4m3"):
    dtype, down = {"e4m3": (ml_dtypes.float8_e4m3fn, 7), "e5m2": (ml_dtypes.float8_e5m2, 14)}[fmt]
    v = np.moveaxis(np.asarray(x, np.float32).astype(ml_dtypes.bfloat16).astype(np.float64), axis, -1)
    blocks = v.reshape(v.shape[:-1] + (-1, 32))
    amax = np.abs(blocks).max(-1, keepdims=True)
    byte = np.maximum(np.where(amax > 0, np.frexp(amax)[1] - 1 + 127, 0) - down, 1)
    scale = np.exp2(byte - 127.0)
    codes = (blocks / scale).astype(np.float32).astype(dtype).astype(np.float64)
    return np.moveaxis((codes * scale).reshape(v.shape), -1, axis)


WIDE = False


def mx_kscale(k):
    if not WIDE:
        return np.ones(k)
    levels = np.array([10, -10, 5, -5, 0])
    a = np.random.permutation(np.resize(levels, k // 512 * 4)).reshape(k // 512, 4)
    idx = np.arange(k)
    return np.exp2(a[idx // 512, idx % 128 // 32])


BF16 = ml_dtypes.bfloat16


def bf(x):
    return np.asarray(x, np.float32).astype(BF16)


def f64(x):
    return np.asarray(x).astype(np.float64)


B, S, D, H, W, F = 4, 1536, 512, 8, 512, 256
EPS = 1e-5


def erf(v):
    a = np.minimum(np.abs(v), 6.0)
    a2 = 2.0 * a * a
    term = a * 1.0
    total = a * 1.0
    for n in range(1, 100):
        term = term * a2 / (2 * n + 1)
        total = total + term
    return np.sign(v) * (2.0 / np.sqrt(np.pi)) * np.exp(-a * a) * total


def gelu_erf(v):
    return 0.5 * v * (1.0 + erf(v / np.sqrt(2.0)))


def setup_inputs():
    s = mx_kscale(D)
    return {"x": bf(np.random.standard_normal((B, S, D))),
            "o_heads": bf(np.random.standard_normal((B, S, D)) * 0.35 * s),
            "Wo": bf(np.random.standard_normal((D, D)) * 2.0 / np.sqrt(D) / s[:, None]),
            "bo": bf(np.random.standard_normal(D) * 0.1),
            "gamma": bf(1.0 + 0.1 * np.random.standard_normal(D)),
            "beta": bf(np.random.standard_normal(D) * 0.1),
            "W1": bf(np.random.standard_normal((D, F)) / np.sqrt(D)),
            "b1": bf(np.random.standard_normal(F) * 0.1)}


def reference(x, o_heads, Wo, bo, gamma, beta, W1, b1):
    attn = (mxq(f64(o_heads), 2, "e4m3") @ mxq(f64(Wo), 0, "e4m3")) + f64(bo)
    r = f64(x) + attn
    mu = r.mean(-1, keepdims=True)
    var = ((r - mu) ** 2).mean(-1, keepdims=True)
    xn = (r - mu) / np.sqrt(var + EPS) * f64(gamma) + f64(beta)
    h = gelu_erf((mxq(xn, 2, "e4m3") @ mxq(f64(W1), 0, "e4m3")) + f64(b1))
    return xn, h

@@ -1,0 +1,301 @@
+from contextlib import ExitStack
+
+import concourse.mybir as mybir
+from concourse.masks import make_identity
+
+F32 = mybir.dt.float32
+BF16 = mybir.dt.bfloat16
+U32 = mybir.dt.uint32
+U8 = mybir.dt.uint8
+FP8X4 = mybir.dt.float8_e4m3fn_x4
+ALU = mybir.AluOpType
+ACT = mybir.ActivationFunctionType
+
+P = 128
+PACK = 4
+D = 512
+F = 256
+TOKENS = 4 * 1536
+PAIR = 2
+ROUNDS = TOKENS // (PAIR * P)
+EPS = 1e-5
+
+FLOPS = 2 * TOKENS * D * (D + F)
+
+
+def tile_swablock_pb_t_kernel(tc, x, o_heads, Wo, bo, gamma, beta, W1, b1, out_0, out_1):
+    nc = tc.nc
+
+    x_rounds = x.flatten_outer_dims().rearrange("(n p t) d -> n p t d", p=P, t=PAIR)
+    o_rounds = o_heads.flatten_outer_dims().rearrange("(n p t) d -> n p t d", p=P, t=PAIR)
+    xn_rounds = out_0.flatten_outer_dims().rearrange("(n p t) d -> n p t d", p=P, t=PAIR)
+    h_rounds = out_1.flatten_outer_dims().rearrange("(n p t) f -> n p t f", p=P, t=PAIR)
+
+    with ExitStack() as ctx:
+        consts = ctx.enter_context(tc.tile_pool(name="consts", bufs=1))
+        loads = ctx.enter_context(tc.tile_pool(name="loads", bufs=5))
+        work = ctx.enter_context(tc.tile_pool(name="work", bufs=3))
+        mx = ctx.enter_context(tc.tile_pool(name="mx", bufs=2))
+        stats = ctx.enter_context(tc.tile_pool(name="stats", bufs=4))
+        stores = ctx.enter_context(tc.tile_pool(name="stores", bufs=4))
+        psum_vec = ctx.enter_context(tc.psum_pool(name="psum_vec", bufs=1))
+        psum_ot = ctx.enter_context(tc.psum_pool(name="psum_ot", bufs=1))
+        psum_attn = ctx.enter_context(tc.psum_pool(name="psum_attn", bufs=2))
+        psum_xt = ctx.enter_context(tc.psum_pool(name="psum_xt", bufs=2))
+        psum_mlp = ctx.enter_context(tc.psum_pool(name="psum_mlp", bufs=1))
+
+        wo_rows = consts.tile([P, PACK, D], BF16)
+        for u in range(2):
+            nc.scalar.dma_start(
+                out=wo_rows[:, 2 * u : 2 * u + 2, :],
+                in_=Wo[256 * u : 256 * u + 256, :].rearrange("(q e) c -> q e c", e=2),
+            )
+        w1_rows = consts.tile([P, PACK, F], BF16)
+        nc.scalar.dma_start(out=w1_rows[:], in_=W1.rearrange("(j q) f -> q j f", q=P))
+
+        wo_grouped = consts.tile([P, D, PACK], BF16, align_bytes=64)
+        nc.vector.tensor_copy(out=wo_grouped[:], in_=wo_rows[:].rearrange("q j c -> q c j"))
+        w1_grouped = consts.tile([P, F, PACK], BF16, align_bytes=64)
+        nc.vector.tensor_copy(out=w1_grouped[:], in_=w1_rows[:].rearrange("q j f -> q f j"))
+        wo_codes = consts.tile([P, D], U32, align_bytes=64)
+        wo_scales = consts.tile([P, D], U8, align_bytes=64)
+        nc.vector.quantize_mx(
+            out=wo_codes[:].bitcast(FP8X4),
+            scales=wo_scales[:],
+            in_=wo_grouped[:].rearrange("q c j -> q (c j)"),
+        )
+        w1_codes = consts.tile([P, F], U32, align_bytes=64)
+        w1_scales = consts.tile([P, F], U8, align_bytes=64)
+        nc.vector.quantize_mx(
+            out=w1_codes[:].bitcast(FP8X4),
+            scales=w1_scales[:],
+            in_=w1_grouped[:].rearrange("q f j -> q (f j)"),
+        )
+
+        vec_rows = consts.tile([P, 4 * D], BF16)
+        nc.vector.memset(vec_rows[:], 0.0)
+        nc.sync.dma_start(out=vec_rows[0:1, 0:D], in_=bo.unsqueeze(0))
+        nc.sync.dma_start(out=vec_rows[0:1, D : 2 * D], in_=gamma.unsqueeze(0))
+        nc.sync.dma_start(out=vec_rows[0:1, 2 * D : 3 * D], in_=beta.unsqueeze(0))
+        for t in range(PAIR):
+            nc.sync.dma_start(out=vec_rows[0:1, 3 * D + t * F : 3 * D + (t + 1) * F], in_=b1.unsqueeze(0))
+        ones = consts.tile([P, P], BF16)
+        nc.vector.memset(ones[:], 1.0)
+
+        gamma_all = psum_vec.tile([P, D], F32)
+        nc.tensor.matmul(out=gamma_all[:], lhsT=ones[:], rhs=vec_rows[:, D : 2 * D], start=True, stop=True)
+        beta_all = psum_vec.tile([P, D], F32)
+        nc.tensor.matmul(out=beta_all[:], lhsT=ones[:], rhs=vec_rows[:, 2 * D : 3 * D], start=True, stop=True)
+        bo_psum = psum_attn.tile([P, D], F32, tag="attn")
+        nc.tensor.matmul(out=bo_psum[:], lhsT=ones[:], rhs=vec_rows[:, 0:D], start=True, stop=True)
+        bo_all = consts.tile([P, D], F32)
+        nc.vector.tensor_copy(out=bo_all[:], in_=bo_psum[:])
+        b1_psum = psum_attn.tile([P, D], F32, tag="attn")
+        nc.tensor.matmul(out=b1_psum[:], lhsT=ones[:], rhs=vec_rows[:, 3 * D : 4 * D], start=True, stop=True)
+        b1_all = consts.tile([P, PAIR * F], F32)
+        nc.vector.tensor_copy(out=b1_all[:], in_=b1_psum[:])
+
+        identity = consts.tile([P, P], F32)
+        make_identity(nc, identity[:])
+        minus_half = consts.tile([P, PAIR], F32)
+        nc.vector.memset(minus_half[:], -0.5)
+
+        kept = [{} for n in range(ROUNDS)]
+
+        def load(n):
+            x_sb = loads.tile([P, PAIR, D], BF16)
+            nc.sync.dma_start(out=x_sb[:], in_=x_rounds[n])
+            o_sb = loads.tile([P, PAIR, D], BF16)
+            nc.sync.dma_start(out=o_sb[:], in_=o_rounds[n])
+            kept[n]["x_sb"] = x_sb
+            kept[n]["o_sb"] = o_sb
+
+        def add_bo(n):
+            x_bo = work.tile([P, PAIR, D], F32, bufs=4)
+            nc.gpsimd.tensor_tensor(
+                out=x_bo[:],
+                in0=kept[n]["x_sb"][:],
+                in1=bo_all[:].unsqueeze(1).to_broadcast([P, PAIR, D]),
+                op=ALU.add,
+            )
+            kept[n]["x_bo"] = x_bo
+
+        def transpose_o(n):
+            o_words = kept[n]["o_sb"][:].bitcast(F32)
+            o_t = psum_ot.tile([P, PAIR, 2, P], F32)
+            for t in range(PAIR):
+                for u in range(2):
+                    nc.tensor.transpose(o_t[:, t, u, :], o_words[:, t, P * u : P * (u + 1)], identity[:])
+            kept[n]["o_t"] = o_t
+
+        def copy_o_t(n):
+            o_grouped = mx.tile([P, PAIR, P, PACK], BF16, align_bytes=64)
+            nc.scalar.copy(
+                out=o_grouped[:].bitcast(F32), in_=kept[n]["o_t"][:].rearrange("q t u r -> q t r u")
+            )
+            kept[n]["o_grouped"] = o_grouped
+
+        def quantise_o(n):
+            o_codes = mx.tile([P, PAIR * P], U32, align_bytes=64)
+            o_scales = mx.tile([P, PAIR * P], U8, align_bytes=64)
+            nc.vector.quantize_mx(
+                out=o_codes[:].bitcast(FP8X4),
+                scales=o_scales[:],
+                in_=kept[n]["o_grouped"][:].rearrange("q t r j -> q (t r j)"),
+            )
+            kept[n]["o_codes"] = o_codes
+            kept[n]["o_scales"] = o_scales
+
+        def attn_matmul(n):
+            for t in range(PAIR):
+                attn = psum_attn.tile([P, D], F32, tag="attn")
+                nc.tensor.matmul_mx(
+                    out=attn[:],
+                    lhsT=kept[n]["o_codes"][:, P * t : P * (t + 1)].bitcast(FP8X4),
+                    lhsT_scale=kept[n]["o_scales"][:, P * t : P * (t + 1)],
+                    rhs=wo_codes[:].bitcast(FP8X4),
+                    rhs_scale=wo_scales[:],
+                    start=True,
+                    stop=True,
+                )
+                kept[n]["attn", t] = attn
+
+        def residual(n):
+            r = work.tile([P, PAIR, D], F32)
+            row_sum = stats.tile([P, PAIR], F32)
+            for t in range(PAIR):
+                nc.vector.scalar_tensor_tensor(
+                    out=r[:, t, :],
+                    in0=kept[n]["attn", t][:],
+                    scalar=1.0,
+                    in1=kept[n]["x_bo"][:, t, :],
+                    op0=ALU.mult,
+                    op1=ALU.add,
+                    accum_out=row_sum[:, t : t + 1],
+                )
+            minus_mean = stats.tile([P, PAIR], F32)
+            nc.scalar.mul(out=minus_mean[:], in_=row_sum[:], mul=-1.0 / D)
+            kept[n]["r"] = r
+            kept[n]["minus_mean"] = minus_mean
+
+        def variance(n):
+            sum_sq = stats.tile([P, PAIR], F32)
+            for t in range(PAIR):
+                squares = work.tile([P, D], BF16)
+                nc.scalar.activation(
+                    out=squares[:],
+                    in_=kept[n]["r"][:, t, :],
+                    func=ACT.Square,
+                    bias=kept[n]["minus_mean"][:, t : t + 1],
+                    scale=1.0,
+                    accum_out=sum_sq[:, t : t + 1],
+                )
+            var_eps = stats.tile([P, PAIR], F32)
+            nc.gpsimd.tensor_scalar(
+                out=var_eps[:], in0=sum_sq[:], scalar1=1.0 / D, scalar2=EPS, op0=ALU.mult, op1=ALU.add
+            )
+            rstd = stats.tile([P, PAIR], F32)
+            nc.gpsimd.tensor_tensor(out=rstd[:], in0=var_eps[:], in1=minus_half[:], op=ALU.pow)
+            kept[n]["rstd"] = rstd
+
+        def centre(n):
+            centred = work.tile([P, PAIR, D], F32)
+            for t in range(PAIR):
+                nc.vector.scalar_tensor_tensor(
+                    out=centred[:, t, :],
+                    in0=kept[n]["r"][:, t, :],
+                    scalar=kept[n]["minus_mean"][:, t : t + 1],
+                    in1=gamma_all[:],
+                    op0=ALU.add,
+                    op1=ALU.mult,
+                )
+            kept[n]["centred"] = centred
+
+        def normalise(n):
+            xn = stores.tile([P, PAIR, D], F32)
+            for t in range(PAIR):
+                nc.vector.scalar_tensor_tensor(
+                    out=xn[:, t, :],
+                    in0=kept[n]["centred"][:, t, :],
+                    scalar=kept[n]["rstd"][:, t : t + 1],
+                    in1=beta_all[:],
+                    op0=ALU.mult,
+                    op1=ALU.add,
+                )
+            nc.sync.dma_start(out=xn_rounds[n], in_=xn[:])
+            kept[n]["xn"] = xn
+
+        def transpose_xn(n):
+            for t in range(PAIR):
+                xn_t = psum_xt.tile([P, PACK, P], F32)
+                for j in range(PACK):
+                    nc.tensor.transpose(xn_t[:, j, :], kept[n]["xn"][:, t, P * j : P * (j + 1)], identity[:])
+                kept[n]["xn_t", t] = xn_t
+
+        def copy_xn_t(n):
+            xn_grouped = mx.tile([P, PAIR, P, PACK], BF16, align_bytes=64)
+            for t in range(PAIR):
+                nc.scalar.copy(
+                    out=xn_grouped[:, t, :, :], in_=kept[n]["xn_t", t][:].rearrange("q j r -> q r j")
+                )
+            kept[n]["xn_grouped"] = xn_grouped
+
+        def quantise_xn(n):
+            xn_codes = mx.tile([P, PAIR * P], U32, align_bytes=64)
+            xn_scales = mx.tile([P, PAIR * P], U8, align_bytes=64)
+            nc.vector.quantize_mx(
+                out=xn_codes[:].bitcast(FP8X4),
+                scales=xn_scales[:],
+                in_=kept[n]["xn_grouped"][:].rearrange("q t r j -> q (t r j)"),
+            )
+            kept[n]["xn_codes"] = xn_codes
+            kept[n]["xn_scales"] = xn_scales
+
+        def mlp_matmul(n):
+            mlp = psum_mlp.tile([P, PAIR * F], F32)
+            for t in range(PAIR):
+                nc.tensor.matmul_mx(
+                    out=mlp[:, F * t : F * (t + 1)],
+                    lhsT=kept[n]["xn_codes"][:, P * t : P * (t + 1)].bitcast(FP8X4),
+                    lhsT_scale=kept[n]["xn_scales"][:, P * t : P * (t + 1)],
+                    rhs=w1_codes[:].bitcast(FP8X4),
+                    rhs_scale=w1_scales[:],
+                    start=True,
+                    stop=True,
+                )
+            kept[n]["mlp"] = mlp
+
+        def add_b1(n):
+            biased = work.tile([P, PAIR * F], F32)
+            nc.vector.tensor_tensor(out=biased[:], in0=kept[n]["mlp"][:], in1=b1_all[:], op=ALU.add)
+            kept[n]["biased"] = biased
+
+        def gelu_store(n):
+            h = stores.tile([P, PAIR, F], F32)
+            nc.scalar.activation(
+                out=h[:].rearrange("p t f -> p (t f)"), in_=kept[n]["biased"][:], func=ACT.Gelu
+            )
+            nc.sync.dma_start(out=h_rounds[n], in_=h[:])
+
+        def step(work_of, n):
+            if 0 <= n < ROUNDS:
+                work_of(n)
+
+        with tc.manual_schedule():
+            for turn in range(-5, ROUNDS + 4):
+                step(load, turn + 5)
+                step(copy_xn_t, turn - 2)
+                step(gelu_store, turn - 4)
+                step(copy_o_t, turn + 2)
+                step(mlp_matmul, turn - 3)
+                step(quantise_o, turn + 1)
+                step(add_bo, turn + 2)
+                step(residual, turn)
+                step(attn_matmul, turn + 1)
+                step(variance, turn)
+                step(normalise, turn - 1)
+                step(transpose_xn, turn - 1)
+                step(transpose_o, turn + 3)
+                step(centre, turn)
+                step(quantise_xn, turn - 2)
+                step(add_b1, turn - 3)

@@ -16,7 +16,9 @@ PACK = 4
 D = 512
 F = 256
 TOKENS = 4 * 1536
+F_TILES = F // P
 PAIR = 2
+ONES_COLS = 64
 ROUNDS = TOKENS // (PAIR * P)
 EPS = 1e-5
 
@@ -39,7 +41,7 @@ def tile_swablock_pb_t_kernel(tc, x, o_heads, Wo, bo, gamma, beta, W1, b1, out_0
         stats = ctx.enter_context(tc.tile_pool(name="stats", bufs=4))
         stores = ctx.enter_context(tc.tile_pool(name="stores", bufs=4))
         psum_vec = ctx.enter_context(tc.psum_pool(name="psum_vec", bufs=1))
-        psum_ot = ctx.enter_context(tc.psum_pool(name="psum_ot", bufs=1))
+        psum_turned = ctx.enter_context(tc.psum_pool(name="psum_turned", bufs=1))
         psum_attn = ctx.enter_context(tc.psum_pool(name="psum_attn", bufs=2))
         psum_xt = ctx.enter_context(tc.psum_pool(name="psum_xt", bufs=2))
         psum_mlp = ctx.enter_context(tc.psum_pool(name="psum_mlp", bufs=1))
@@ -72,13 +74,12 @@ def tile_swablock_pb_t_kernel(tc, x, o_heads, Wo, bo, gamma, beta, W1, b1, out_0
             in_=w1_grouped[:].rearrange("q f j -> q (f j)"),
         )
 
-        vec_rows = consts.tile([P, 4 * D], BF16)
+        vec_rows = consts.tile([P, 3 * D + F], BF16)
         nc.vector.memset(vec_rows[:], 0.0)
         nc.sync.dma_start(out=vec_rows[0:1, 0:D], in_=bo.unsqueeze(0))
         nc.sync.dma_start(out=vec_rows[0:1, D : 2 * D], in_=gamma.unsqueeze(0))
         nc.sync.dma_start(out=vec_rows[0:1, 2 * D : 3 * D], in_=beta.unsqueeze(0))
-        for t in range(PAIR):
-            nc.sync.dma_start(out=vec_rows[0:1, 3 * D + t * F : 3 * D + (t + 1) * F], in_=b1.unsqueeze(0))
+        nc.sync.dma_start(out=vec_rows[0:1, 3 * D : 3 * D + F], in_=b1.unsqueeze(0))
         ones = consts.tile([P, P], BF16)
         nc.vector.memset(ones[:], 1.0)
 
@@ -90,10 +91,17 @@ def tile_swablock_pb_t_kernel(tc, x, o_heads, Wo, bo, gamma, beta, W1, b1, out_0
         nc.tensor.matmul(out=bo_psum[:], lhsT=ones[:], rhs=vec_rows[:, 0:D], start=True, stop=True)
         bo_all = consts.tile([P, D], F32)
         nc.vector.tensor_copy(out=bo_all[:], in_=bo_psum[:])
-        b1_psum = psum_attn.tile([P, D], F32, tag="attn")
-        nc.tensor.matmul(out=b1_psum[:], lhsT=ones[:], rhs=vec_rows[:, 3 * D : 4 * D], start=True, stop=True)
-        b1_all = consts.tile([P, PAIR * F], F32)
-        nc.vector.tensor_copy(out=b1_all[:], in_=b1_psum[:])
+        b1_psum = psum_attn.tile([P, F_TILES, ONES_COLS], F32, tag="attn")
+        for c in range(F_TILES):
+            nc.tensor.matmul(
+                out=b1_psum[:, c, :],
+                lhsT=vec_rows[:, 3 * D + P * c : 3 * D + P * (c + 1)],
+                rhs=ones[:, 0:ONES_COLS],
+                start=True,
+                stop=True,
+            )
+        b1_column = consts.tile([P, F_TILES], F32)
+        nc.vector.tensor_copy(out=b1_column[:], in_=b1_psum[:, :, 0])
 
         identity = consts.tile([P, P], F32)
         make_identity(nc, identity[:])
@@ -122,7 +130,7 @@ def tile_swablock_pb_t_kernel(tc, x, o_heads, Wo, bo, gamma, beta, W1, b1, out_0
 
         def transpose_o(n):
             o_words = kept[n]["o_sb"][:].bitcast(F32)
-            o_t = psum_ot.tile([P, PAIR, 2, P], F32)
+            o_t = psum_turned.tile([P, PAIR, 2, P], F32, tag="turned")
             for t in range(PAIR):
                 for u in range(2):
                     nc.tensor.transpose(o_t[:, t, u, :], o_words[:, t, P * u : P * (u + 1)], identity[:])
@@ -252,29 +260,43 @@ def tile_swablock_pb_t_kernel(tc, x, o_heads, Wo, bo, gamma, beta, W1, b1, out_0
             kept[n]["xn_scales"] = xn_scales
 
         def mlp_matmul(n):
-            mlp = psum_mlp.tile([P, PAIR * F], F32)
-            for t in range(PAIR):
+            mlp_t = psum_mlp.tile([P, F_TILES, PAIR * P], F32)
+            for c in range(F_TILES):
                 nc.tensor.matmul_mx(
-                    out=mlp[:, F * t : F * (t + 1)],
-                    lhsT=kept[n]["xn_codes"][:, P * t : P * (t + 1)].bitcast(FP8X4),
-                    lhsT_scale=kept[n]["xn_scales"][:, P * t : P * (t + 1)],
-                    rhs=w1_codes[:].bitcast(FP8X4),
-                    rhs_scale=w1_scales[:],
+                    out=mlp_t[:, c, :],
+                    lhsT=w1_codes[:, P * c : P * (c + 1)].bitcast(FP8X4),
+                    lhsT_scale=w1_scales[:, P * c : P * (c + 1)],
+                    rhs=kept[n]["xn_codes"][:].bitcast(FP8X4),
+                    rhs_scale=kept[n]["xn_scales"][:],
                     start=True,
                     stop=True,
                 )
-            kept[n]["mlp"] = mlp
+            kept[n]["mlp_t"] = mlp_t
 
-        def add_b1(n):
-            biased = work.tile([P, PAIR * F], F32)
-            nc.vector.tensor_tensor(out=biased[:], in0=kept[n]["mlp"][:], in1=b1_all[:], op=ALU.add)
-            kept[n]["biased"] = biased
+        def gelu(n):
+            h_t = work.tile([P, F_TILES, PAIR * P], F32)
+            for c in range(F_TILES):
+                nc.scalar.activation(
+                    out=h_t[:, c, :],
+                    in_=kept[n]["mlp_t"][:, c, :],
+                    func=ACT.Gelu,
+                    bias=b1_column[:, c : c + 1],
+                    scale=1.0,
+                )
+            kept[n]["h_t"] = h_t
 
-        def gelu_store(n):
+        def transpose_h(n):
+            h_psum = psum_turned.tile([P, PAIR, F_TILES, P], F32, tag="turned")
+            for t in range(PAIR):
+                for c in range(F_TILES):
+                    nc.tensor.transpose(
+                        h_psum[:, t, c, :], kept[n]["h_t"][:, c, P * t : P * (t + 1)], identity[:]
+                    )
+            kept[n]["h_psum"] = h_psum
+
+        def copy_h(n):
             h = stores.tile([P, PAIR, F], F32)
-            nc.scalar.activation(
-                out=h[:].rearrange("p t f -> p (t f)"), in_=kept[n]["biased"][:], func=ACT.Gelu
-            )
+            nc.scalar.copy(out=h[:], in_=kept[n]["h_psum"][:].rearrange("p t c f -> p t (c f)"))
             nc.sync.dma_start(out=h_rounds[n], in_=h[:])
 
         def step(work_of, n):
@@ -284,18 +306,19 @@ def tile_swablock_pb_t_kernel(tc, x, o_heads, Wo, bo, gamma, beta, W1, b1, out_0
         with tc.manual_schedule():
             for turn in range(-5, ROUNDS + 4):
                 step(load, turn + 5)
-                step(copy_xn_t, turn - 2)
-                step(gelu_store, turn - 4)
                 step(copy_o_t, turn + 2)
+                step(transpose_h, turn - 4)
+                step(copy_xn_t, turn - 2)
+                step(copy_h, turn - 4)
                 step(mlp_matmul, turn - 3)
                 step(quantise_o, turn + 1)
                 step(add_bo, turn + 2)
                 step(residual, turn)
                 step(attn_matmul, turn + 1)
                 step(variance, turn)
+                step(gelu, turn - 3)
                 step(normalise, turn - 1)
                 step(transpose_xn, turn - 1)
                 step(transpose_o, turn + 3)
                 step(centre, turn)
                 step(quantise_xn, turn - 2)
-                step(add_b1, turn - 3)

@@ -46,19 +46,26 @@ def tile_swablock_pb_t_kernel(tc, x, o_heads, Wo, bo, gamma, beta, W1, b1, out_0
         psum_xt = ctx.enter_context(tc.psum_pool(name="psum_xt", bufs=2))
         psum_mlp = ctx.enter_context(tc.psum_pool(name="psum_mlp", bufs=1))
 
+        kept = [{} for n in range(ROUNDS)]
+
+        def load(n):
+            o_sb = loads.tile([P, PAIR, D], BF16)
+            nc.sync.dma_start(out=o_sb[:], in_=o_rounds[n])
+            x_sb = loads.tile([P, PAIR, D], BF16)
+            nc.sync.dma_start(out=x_sb[:], in_=x_rounds[n])
+            kept[n]["o_sb"] = o_sb
+            kept[n]["x_sb"] = x_sb
+
+        load(0)
+
         wo_rows = consts.tile([P, PACK, D], BF16)
         for u in range(2):
             nc.scalar.dma_start(
                 out=wo_rows[:, 2 * u : 2 * u + 2, :],
                 in_=Wo[256 * u : 256 * u + 256, :].rearrange("(q e) c -> q e c", e=2),
             )
-        w1_rows = consts.tile([P, PACK, F], BF16)
-        nc.scalar.dma_start(out=w1_rows[:], in_=W1.rearrange("(j q) f -> q j f", q=P))
-
         wo_grouped = consts.tile([P, D, PACK], BF16, align_bytes=64)
         nc.vector.tensor_copy(out=wo_grouped[:], in_=wo_rows[:].rearrange("q j c -> q c j"))
-        w1_grouped = consts.tile([P, F, PACK], BF16, align_bytes=64)
-        nc.vector.tensor_copy(out=w1_grouped[:], in_=w1_rows[:].rearrange("q j f -> q f j"))
         wo_codes = consts.tile([P, D], U32, align_bytes=64)
         wo_scales = consts.tile([P, D], U8, align_bytes=64)
         nc.vector.quantize_mx(
@@ -66,14 +73,6 @@ def tile_swablock_pb_t_kernel(tc, x, o_heads, Wo, bo, gamma, beta, W1, b1, out_0
             scales=wo_scales[:],
             in_=wo_grouped[:].rearrange("q c j -> q (c j)"),
         )
-        w1_codes = consts.tile([P, F], U32, align_bytes=64)
-        w1_scales = consts.tile([P, F], U8, align_bytes=64)
-        nc.vector.quantize_mx(
-            out=w1_codes[:].bitcast(FP8X4),
-            scales=w1_scales[:],
-            in_=w1_grouped[:].rearrange("q f j -> q (f j)"),
-        )
-
         vec_rows = consts.tile([P, 3 * D + F], BF16)
         nc.vector.memset(vec_rows[:], 0.0)
         nc.sync.dma_start(out=vec_rows[0:1, 0:D], in_=bo.unsqueeze(0))
@@ -83,14 +82,14 @@ def tile_swablock_pb_t_kernel(tc, x, o_heads, Wo, bo, gamma, beta, W1, b1, out_0
         ones = consts.tile([P, P], BF16)
         nc.vector.memset(ones[:], 1.0)
 
+        bo_psum = psum_attn.tile([P, D], F32, tag="attn")
+        nc.tensor.matmul(out=bo_psum[:], lhsT=ones[:], rhs=vec_rows[:, 0:D], start=True, stop=True)
+        bo_all = consts.tile([P, D], F32)
+        nc.scalar.copy(out=bo_all[:], in_=bo_psum[:])
         gamma_all = psum_vec.tile([P, D], F32)
         nc.tensor.matmul(out=gamma_all[:], lhsT=ones[:], rhs=vec_rows[:, D : 2 * D], start=True, stop=True)
         beta_all = psum_vec.tile([P, D], F32)
         nc.tensor.matmul(out=beta_all[:], lhsT=ones[:], rhs=vec_rows[:, 2 * D : 3 * D], start=True, stop=True)
-        bo_psum = psum_attn.tile([P, D], F32, tag="attn")
-        nc.tensor.matmul(out=bo_psum[:], lhsT=ones[:], rhs=vec_rows[:, 0:D], start=True, stop=True)
-        bo_all = consts.tile([P, D], F32)
-        nc.vector.tensor_copy(out=bo_all[:], in_=bo_psum[:])
         b1_psum = psum_attn.tile([P, F_TILES, ONES_COLS], F32, tag="attn")
         for c in range(F_TILES):
             nc.tensor.matmul(
@@ -101,31 +100,30 @@ def tile_swablock_pb_t_kernel(tc, x, o_heads, Wo, bo, gamma, beta, W1, b1, out_0
                 stop=True,
             )
         b1_column = consts.tile([P, F_TILES], F32)
-        nc.vector.tensor_copy(out=b1_column[:], in_=b1_psum[:, :, 0])
+        nc.scalar.copy(out=b1_column[:], in_=b1_psum[:, :, 0])
 
         identity = consts.tile([P, P], F32)
         make_identity(nc, identity[:])
         minus_half = consts.tile([P, PAIR], F32)
         nc.vector.memset(minus_half[:], -0.5)
 
-        kept = [{} for n in range(ROUNDS)]
+        w1_rows = consts.tile([P, PACK, F], BF16)
+        nc.scalar.dma_start(out=w1_rows[:], in_=W1.rearrange("(j q) f -> q j f", q=P))
+        w1_grouped = consts.tile([P, F, PACK], BF16, align_bytes=64)
+        nc.scalar.copy(out=w1_grouped[:], in_=w1_rows[:].rearrange("q j f -> q f j"))
+        w1_codes = consts.tile([P, F], U32, align_bytes=64)
+        w1_scales = consts.tile([P, F], U8, align_bytes=64)
+        nc.vector.quantize_mx(
+            out=w1_codes[:].bitcast(FP8X4),
+            scales=w1_scales[:],
+            in_=w1_grouped[:].rearrange("q f j -> q (f j)"),
+        )
 
-        def load(n):
-            x_sb = loads.tile([P, PAIR, D], BF16)
-            nc.sync.dma_start(out=x_sb[:], in_=x_rounds[n])
-            o_sb = loads.tile([P, PAIR, D], BF16)
-            nc.sync.dma_start(out=o_sb[:], in_=o_rounds[n])
-            kept[n]["x_sb"] = x_sb
-            kept[n]["o_sb"] = o_sb
 
         def add_bo(n):
             x_bo = work.tile([P, PAIR, D], F32, bufs=4)
-            nc.gpsimd.tensor_tensor(
-                out=x_bo[:],
-                in0=kept[n]["x_sb"][:],
-                in1=bo_all[:].unsqueeze(1).to_broadcast([P, PAIR, D]),
-                op=ALU.add,
-            )
+            for t in range(PAIR):
+                nc.gpsimd.tensor_tensor(out=x_bo[:, t, :], in0=kept[n]["x_sb"][:, t, :], in1=bo_all[:], op=ALU.add)
             kept[n]["x_bo"] = x_bo
 
         def transpose_o(n):
@@ -304,17 +302,17 @@ def tile_swablock_pb_t_kernel(tc, x, o_heads, Wo, bo, gamma, beta, W1, b1, out_0
                 work_of(n)
 
         with tc.manual_schedule():
-            for turn in range(-5, ROUNDS + 4):
+            for turn in range(-4, ROUNDS + 5):
                 step(load, turn + 5)
                 step(copy_o_t, turn + 2)
-                step(transpose_h, turn - 4)
+                step(transpose_h, turn - 5)
                 step(copy_xn_t, turn - 2)
-                step(copy_h, turn - 4)
                 step(mlp_matmul, turn - 3)
                 step(quantise_o, turn + 1)
                 step(add_bo, turn + 2)
                 step(residual, turn)
                 step(attn_matmul, turn + 1)
+                step(copy_h, turn - 5)
                 step(variance, turn)
                 step(gelu, turn - 3)
                 step(normalise, turn - 1)

@@ -84,8 +84,9 @@ def tile_swablock_pb_t_kernel(tc, x, o_heads, Wo, bo, gamma, beta, W1, b1, out_0
 
         bo_psum = psum_attn.tile([P, D], F32, tag="attn")
         nc.tensor.matmul(out=bo_psum[:], lhsT=ones[:], rhs=vec_rows[:, 0:D], start=True, stop=True)
-        bo_all = consts.tile([P, D], F32)
-        nc.scalar.copy(out=bo_all[:], in_=bo_psum[:])
+        bo_all = consts.tile([P, PAIR, D], F32)
+        for t in range(PAIR):
+            nc.scalar.copy(out=bo_all[:, t, :], in_=bo_psum[:])
         gamma_all = psum_vec.tile([P, D], F32)
         nc.tensor.matmul(out=gamma_all[:], lhsT=ones[:], rhs=vec_rows[:, D : 2 * D], start=True, stop=True)
         beta_all = psum_vec.tile([P, D], F32)
@@ -122,8 +123,7 @@ def tile_swablock_pb_t_kernel(tc, x, o_heads, Wo, bo, gamma, beta, W1, b1, out_0
 
         def add_bo(n):
             x_bo = work.tile([P, PAIR, D], F32, bufs=4)
-            for t in range(PAIR):
-                nc.gpsimd.tensor_tensor(out=x_bo[:, t, :], in0=kept[n]["x_sb"][:, t, :], in1=bo_all[:], op=ALU.add)
+            nc.gpsimd.tensor_tensor(out=x_bo[:], in0=kept[n]["x_sb"][:], in1=bo_all[:], op=ALU.add)
             kept[n]["x_bo"] = x_bo
 
         def transpose_o(n):
@@ -196,9 +196,12 @@ def tile_swablock_pb_t_kernel(tc, x, o_heads, Wo, bo, gamma, beta, W1, b1, out_0
                     scale=1.0,
                     accum_out=sum_sq[:, t : t + 1],
                 )
+            kept[n]["sum_sq"] = sum_sq
+
+        def inverse_deviation(n):
             var_eps = stats.tile([P, PAIR], F32)
-            nc.gpsimd.tensor_scalar(
-                out=var_eps[:], in0=sum_sq[:], scalar1=1.0 / D, scalar2=EPS, op0=ALU.mult, op1=ALU.add
+            nc.scalar.activation(
+                out=var_eps[:], in_=kept[n]["sum_sq"][:], func=ACT.Identity, scale=1.0 / D, bias=EPS
             )
             rstd = stats.tile([P, PAIR], F32)
             nc.gpsimd.tensor_tensor(out=rstd[:], in0=var_eps[:], in1=minus_half[:], op=ALU.pow)
@@ -315,6 +318,7 @@ def tile_swablock_pb_t_kernel(tc, x, o_heads, Wo, bo, gamma, beta, W1, b1, out_0
                 step(copy_h, turn - 5)
                 step(variance, turn)
                 step(gelu, turn - 3)
+                step(inverse_deviation, turn)
                 step(normalise, turn - 1)
                 step(transpose_xn, turn - 1)
                 step(transpose_o, turn + 3)

@@ -41,7 +41,8 @@ def tile_swablock_pb_t_kernel(tc, x, o_heads, Wo, bo, gamma, beta, W1, b1, out_0
         stats = ctx.enter_context(tc.tile_pool(name="stats", bufs=4))
         stores = ctx.enter_context(tc.tile_pool(name="stores", bufs=4))
         psum_vec = ctx.enter_context(tc.psum_pool(name="psum_vec", bufs=1))
-        psum_turned = ctx.enter_context(tc.psum_pool(name="psum_turned", bufs=1))
+        psum_o = ctx.enter_context(tc.psum_pool(name="psum_o", bufs=1))
+        psum_h = ctx.enter_context(tc.psum_pool(name="psum_h", bufs=1))
         psum_attn = ctx.enter_context(tc.psum_pool(name="psum_attn", bufs=2))
         psum_xt = ctx.enter_context(tc.psum_pool(name="psum_xt", bufs=2))
         psum_mlp = ctx.enter_context(tc.psum_pool(name="psum_mlp", bufs=1))
@@ -87,10 +88,17 @@ def tile_swablock_pb_t_kernel(tc, x, o_heads, Wo, bo, gamma, beta, W1, b1, out_0
         bo_all = consts.tile([P, PAIR, D], F32)
         for t in range(PAIR):
             nc.scalar.copy(out=bo_all[:, t, :], in_=bo_psum[:])
-        gamma_all = psum_vec.tile([P, D], F32)
-        nc.tensor.matmul(out=gamma_all[:], lhsT=ones[:], rhs=vec_rows[:, D : 2 * D], start=True, stop=True)
-        beta_all = psum_vec.tile([P, D], F32)
-        nc.tensor.matmul(out=beta_all[:], lhsT=ones[:], rhs=vec_rows[:, 2 * D : 3 * D], start=True, stop=True)
+        gamma_beta = psum_vec.tile([P, 2, D], BF16)
+        for i in range(2):
+            nc.tensor.matmul(
+                out=gamma_beta[:, i, :],
+                lhsT=ones[:],
+                rhs=vec_rows[:, (1 + i) * D : (2 + i) * D],
+                start=True,
+                stop=True,
+            )
+        gamma_all = gamma_beta[:, 0, :]
+        beta_all = gamma_beta[:, 1, :]
         b1_psum = psum_attn.tile([P, F_TILES, ONES_COLS], F32, tag="attn")
         for c in range(F_TILES):
             nc.tensor.matmul(
@@ -128,7 +136,7 @@ def tile_swablock_pb_t_kernel(tc, x, o_heads, Wo, bo, gamma, beta, W1, b1, out_0
 
         def transpose_o(n):
             o_words = kept[n]["o_sb"][:].bitcast(F32)
-            o_t = psum_turned.tile([P, PAIR, 2, P], F32, tag="turned")
+            o_t = psum_o.tile([P, PAIR, 2, P], F32)
             for t in range(PAIR):
                 for u in range(2):
                     nc.tensor.transpose(o_t[:, t, u, :], o_words[:, t, P * u : P * (u + 1)], identity[:])
@@ -214,7 +222,7 @@ def tile_swablock_pb_t_kernel(tc, x, o_heads, Wo, bo, gamma, beta, W1, b1, out_0
                     out=centred[:, t, :],
                     in0=kept[n]["r"][:, t, :],
                     scalar=kept[n]["minus_mean"][:, t : t + 1],
-                    in1=gamma_all[:],
+                    in1=gamma_all,
                     op0=ALU.add,
                     op1=ALU.mult,
                 )
@@ -227,7 +235,7 @@ def tile_swablock_pb_t_kernel(tc, x, o_heads, Wo, bo, gamma, beta, W1, b1, out_0
                     out=xn[:, t, :],
                     in0=kept[n]["centred"][:, t, :],
                     scalar=kept[n]["rstd"][:, t : t + 1],
-                    in1=beta_all[:],
+                    in1=beta_all,
                     op0=ALU.mult,
                     op1=ALU.add,
                 )
@@ -287,7 +295,7 @@ def tile_swablock_pb_t_kernel(tc, x, o_heads, Wo, bo, gamma, beta, W1, b1, out_0
             kept[n]["h_t"] = h_t
 
         def transpose_h(n):
-            h_psum = psum_turned.tile([P, PAIR, F_TILES, P], F32, tag="turned")
+            h_psum = psum_h.tile([P, PAIR, F_TILES, P], F32)
             for t in range(PAIR):
                 for c in range(F_TILES):
                     nc.tensor.transpose(

@@ -19,7 +19,8 @@ TOKENS = 4 * 1536
 F_TILES = F // P
 PAIR = 2
 ONES_COLS = 64
-ROUNDS = TOKENS // (PAIR * P)
+SIZES = [1] + [PAIR] * (TOKENS // (PAIR * P) - 1) + [1]
+ROUNDS = len(SIZES)
 EPS = 1e-5
 
 FLOPS = 2 * TOKENS * D * (D + F)
@@ -28,10 +29,10 @@ FLOPS = 2 * TOKENS * D * (D + F)
 def tile_swablock_pb_t_kernel(tc, x, o_heads, Wo, bo, gamma, beta, W1, b1, out_0, out_1):
     nc = tc.nc
 
-    x_rounds = x.flatten_outer_dims().rearrange("(n p t) d -> n p t d", p=P, t=PAIR)
-    o_rounds = o_heads.flatten_outer_dims().rearrange("(n p t) d -> n p t d", p=P, t=PAIR)
-    xn_rounds = out_0.flatten_outer_dims().rearrange("(n p t) d -> n p t d", p=P, t=PAIR)
-    h_rounds = out_1.flatten_outer_dims().rearrange("(n p t) f -> n p t f", p=P, t=PAIR)
+    def round_of(tensor, n):
+        first = P * sum(SIZES[:n])
+        rows = tensor.flatten_outer_dims()[first : first + P * SIZES[n], :]
+        return rows.rearrange("(p t) d -> p t d", p=P, t=SIZES[n])
 
     with ExitStack() as ctx:
         consts = ctx.enter_context(tc.tile_pool(name="consts", bufs=1))
@@ -49,15 +50,28 @@ def tile_swablock_pb_t_kernel(tc, x, o_heads, Wo, bo, gamma, beta, W1, b1, out_0
 
         kept = [{} for n in range(ROUNDS)]
 
-        def load(n):
+        def load_o(n):
             o_sb = loads.tile([P, PAIR, D], BF16)
-            nc.sync.dma_start(out=o_sb[:], in_=o_rounds[n])
-            x_sb = loads.tile([P, PAIR, D], BF16)
-            nc.sync.dma_start(out=x_sb[:], in_=x_rounds[n])
+            nc.sync.dma_start(out=o_sb[:, 0 : SIZES[n], :], in_=round_of(o_heads, n))
             kept[n]["o_sb"] = o_sb
+
+        def load_x(n):
+            x_sb = loads.tile([P, PAIR, D], BF16)
+            nc.sync.dma_start(out=x_sb[:, 0 : SIZES[n], :], in_=round_of(x, n))
             kept[n]["x_sb"] = x_sb
 
-        load(0)
+        bo_row = consts.tile([P, D], BF16)
+        nc.vector.memset(bo_row[:], 0.0)
+        vec_rows = consts.tile([P, 2 * D + F], BF16)
+        nc.vector.memset(vec_rows[:], 0.0)
+        minus_half = consts.tile([P, PAIR], F32)
+        nc.vector.memset(minus_half[:], -0.5)
+        ones = consts.tile([P, P], BF16)
+        nc.vector.memset(ones[:], 1.0)
+        identity = consts.tile([P, P], F32)
+        make_identity(nc, identity[:])
+        gelu_warm = consts.tile([P, 1], F32)
+        nc.scalar.activation(out=gelu_warm[:], in_=minus_half[:, 0:1], func=ACT.Gelu, bias=0.0, scale=1.0)
 
         wo_rows = consts.tile([P, PACK, D], BF16)
         for u in range(2):
@@ -65,79 +79,85 @@ def tile_swablock_pb_t_kernel(tc, x, o_heads, Wo, bo, gamma, beta, W1, b1, out_0
                 out=wo_rows[:, 2 * u : 2 * u + 2, :],
                 in_=Wo[256 * u : 256 * u + 256, :].rearrange("(q e) c -> q e c", e=2),
             )
+        load_o(0)
+        nc.sync.dma_start(out=bo_row[0:1, :], in_=bo.unsqueeze(0))
+        load_x(0)
+        nc.sync.dma_start(out=vec_rows[0:1, 0:D], in_=gamma.unsqueeze(0))
+        nc.sync.dma_start(out=vec_rows[0:1, D : 2 * D], in_=beta.unsqueeze(0))
+        nc.sync.dma_start(out=vec_rows[0:1, 2 * D : 2 * D + F], in_=b1.unsqueeze(0))
+        load_o(1)
+        load_x(1)
+        w1_rows = consts.tile([P, PACK, F], BF16)
+        nc.sync.dma_start(out=w1_rows[:], in_=W1.rearrange("(j q) f -> q j f", q=P))
+
         wo_grouped = consts.tile([P, D, PACK], BF16, align_bytes=64)
-        nc.vector.tensor_copy(out=wo_grouped[:], in_=wo_rows[:].rearrange("q j c -> q c j"))
         wo_codes = consts.tile([P, D], U32, align_bytes=64)
         wo_scales = consts.tile([P, D], U8, align_bytes=64)
-        nc.vector.quantize_mx(
-            out=wo_codes[:].bitcast(FP8X4),
-            scales=wo_scales[:],
-            in_=wo_grouped[:].rearrange("q c j -> q (c j)"),
-        )
-        vec_rows = consts.tile([P, 3 * D + F], BF16)
-        nc.vector.memset(vec_rows[:], 0.0)
-        nc.sync.dma_start(out=vec_rows[0:1, 0:D], in_=bo.unsqueeze(0))
-        nc.sync.dma_start(out=vec_rows[0:1, D : 2 * D], in_=gamma.unsqueeze(0))
-        nc.sync.dma_start(out=vec_rows[0:1, 2 * D : 3 * D], in_=beta.unsqueeze(0))
-        nc.sync.dma_start(out=vec_rows[0:1, 3 * D : 3 * D + F], in_=b1.unsqueeze(0))
-        ones = consts.tile([P, P], BF16)
-        nc.vector.memset(ones[:], 1.0)
-
-        bo_psum = psum_attn.tile([P, D], F32, tag="attn")
-        nc.tensor.matmul(out=bo_psum[:], lhsT=ones[:], rhs=vec_rows[:, 0:D], start=True, stop=True)
-        bo_all = consts.tile([P, PAIR, D], F32)
-        for t in range(PAIR):
-            nc.scalar.copy(out=bo_all[:, t, :], in_=bo_psum[:])
-        gamma_beta = psum_vec.tile([P, 2, D], BF16)
-        for i in range(2):
-            nc.tensor.matmul(
-                out=gamma_beta[:, i, :],
-                lhsT=ones[:],
-                rhs=vec_rows[:, (1 + i) * D : (2 + i) * D],
-                start=True,
-                stop=True,
-            )
-        gamma_all = gamma_beta[:, 0, :]
-        beta_all = gamma_beta[:, 1, :]
-        b1_psum = psum_attn.tile([P, F_TILES, ONES_COLS], F32, tag="attn")
-        for c in range(F_TILES):
-            nc.tensor.matmul(
-                out=b1_psum[:, c, :],
-                lhsT=vec_rows[:, 3 * D + P * c : 3 * D + P * (c + 1)],
-                rhs=ones[:, 0:ONES_COLS],
-                start=True,
-                stop=True,
-            )
-        b1_column = consts.tile([P, F_TILES], F32)
-        nc.scalar.copy(out=b1_column[:], in_=b1_psum[:, :, 0])
-
-        identity = consts.tile([P, P], F32)
-        make_identity(nc, identity[:])
-        minus_half = consts.tile([P, PAIR], F32)
-        nc.vector.memset(minus_half[:], -0.5)
-
-        w1_rows = consts.tile([P, PACK, F], BF16)
-        nc.scalar.dma_start(out=w1_rows[:], in_=W1.rearrange("(j q) f -> q j f", q=P))
         w1_grouped = consts.tile([P, F, PACK], BF16, align_bytes=64)
-        nc.scalar.copy(out=w1_grouped[:], in_=w1_rows[:].rearrange("q j f -> q f j"))
         w1_codes = consts.tile([P, F], U32, align_bytes=64)
         w1_scales = consts.tile([P, F], U8, align_bytes=64)
-        nc.vector.quantize_mx(
-            out=w1_codes[:].bitcast(FP8X4),
-            scales=w1_scales[:],
-            in_=w1_grouped[:].rearrange("q f j -> q (f j)"),
-        )
+
+        def quantise_wo():
+            nc.vector.tensor_copy(out=wo_grouped[:], in_=wo_rows[:].rearrange("q j c -> q c j"))
+            nc.vector.quantize_mx(
+                out=wo_codes[:].bitcast(FP8X4),
+                scales=wo_scales[:],
+                in_=wo_grouped[:].rearrange("q c j -> q (c j)"),
+            )
+
+        def quantise_w1():
+            nc.scalar.copy(out=w1_grouped[:], in_=w1_rows[:].rearrange("q j f -> q f j"))
+            nc.vector.quantize_mx(
+                out=w1_codes[:].bitcast(FP8X4),
+                scales=w1_scales[:],
+                in_=w1_grouped[:].rearrange("q f j -> q (f j)"),
+            )
+
+        bo_all = consts.tile([P, PAIR, D], F32)
+        gamma_beta = psum_vec.tile([P, 2, D], BF16)
+        gamma_all = gamma_beta[:, 0, :]
+        beta_all = gamma_beta[:, 1, :]
+        b1_column = consts.tile([P, F_TILES], F32)
+
+        def spread_bo():
+            bo_psum = psum_attn.tile([P, D], F32, tag="attn")
+            nc.tensor.matmul(out=bo_psum[:], lhsT=ones[:], rhs=bo_row[:], start=True, stop=True)
+            for t in range(PAIR):
+                nc.scalar.copy(out=bo_all[:, t, :], in_=bo_psum[:])
+
+        def spread_others():
+            for i in range(2):
+                nc.tensor.matmul(
+                    out=gamma_beta[:, i, :],
+                    lhsT=ones[:],
+                    rhs=vec_rows[:, i * D : (i + 1) * D],
+                    start=True,
+                    stop=True,
+                )
+            b1_psum = psum_mlp.tile([P, F_TILES, PAIR * P], F32, tag="mlp_t")
+            for c in range(F_TILES):
+                nc.tensor.matmul(
+                    out=b1_psum[:, c, 0:ONES_COLS],
+                    lhsT=vec_rows[:, 2 * D + P * c : 2 * D + P * (c + 1)],
+                    rhs=ones[:, 0:ONES_COLS],
+                    start=True,
+                    stop=True,
+                )
+            nc.scalar.copy(out=b1_column[:], in_=b1_psum[:, :, 0])
 
 
         def add_bo(n):
             x_bo = work.tile([P, PAIR, D], F32, bufs=4)
-            nc.gpsimd.tensor_tensor(out=x_bo[:], in0=kept[n]["x_sb"][:], in1=bo_all[:], op=ALU.add)
+            s = SIZES[n]
+            nc.gpsimd.tensor_tensor(
+                out=x_bo[:, 0:s, :], in0=kept[n]["x_sb"][:, 0:s, :], in1=bo_all[:, 0:s, :], op=ALU.add
+            )
             kept[n]["x_bo"] = x_bo
 
         def transpose_o(n):
             o_words = kept[n]["o_sb"][:].bitcast(F32)
             o_t = psum_o.tile([P, PAIR, 2, P], F32)
-            for t in range(PAIR):
+            for t in range(SIZES[n]):
                 for u in range(2):
                     nc.tensor.transpose(o_t[:, t, u, :], o_words[:, t, P * u : P * (u + 1)], identity[:])
             kept[n]["o_t"] = o_t
@@ -145,7 +165,8 @@ def tile_swablock_pb_t_kernel(tc, x, o_heads, Wo, bo, gamma, beta, W1, b1, out_0
         def copy_o_t(n):
             o_grouped = mx.tile([P, PAIR, P, PACK], BF16, align_bytes=64)
             nc.scalar.copy(
-                out=o_grouped[:].bitcast(F32), in_=kept[n]["o_t"][:].rearrange("q t u r -> q t r u")
+                out=o_grouped[:, 0 : SIZES[n], :, :].bitcast(F32),
+                in_=kept[n]["o_t"][:, 0 : SIZES[n], :, :].rearrange("q t u r -> q t r u"),
             )
             kept[n]["o_grouped"] = o_grouped
 
@@ -153,15 +174,15 @@ def tile_swablock_pb_t_kernel(tc, x, o_heads, Wo, bo, gamma, beta, W1, b1, out_0
             o_codes = mx.tile([P, PAIR * P], U32, align_bytes=64)
             o_scales = mx.tile([P, PAIR * P], U8, align_bytes=64)
             nc.vector.quantize_mx(
-                out=o_codes[:].bitcast(FP8X4),
-                scales=o_scales[:],
-                in_=kept[n]["o_grouped"][:].rearrange("q t r j -> q (t r j)"),
+                out=o_codes[:, 0 : P * SIZES[n]].bitcast(FP8X4),
+                scales=o_scales[:, 0 : P * SIZES[n]],
+                in_=kept[n]["o_grouped"][:, 0 : SIZES[n], :, :].rearrange("q t r j -> q (t r j)"),
             )
             kept[n]["o_codes"] = o_codes
             kept[n]["o_scales"] = o_scales
 
         def attn_matmul(n):
-            for t in range(PAIR):
+            for t in range(SIZES[n]):
                 attn = psum_attn.tile([P, D], F32, tag="attn")
                 nc.tensor.matmul_mx(
                     out=attn[:],
@@ -177,7 +198,7 @@ def tile_swablock_pb_t_kernel(tc, x, o_heads, Wo, bo, gamma, beta, W1, b1, out_0
         def residual(n):
             r = work.tile([P, PAIR, D], F32)
             row_sum = stats.tile([P, PAIR], F32)
-            for t in range(PAIR):
+            for t in range(SIZES[n]):
                 nc.vector.scalar_tensor_tensor(
                     out=r[:, t, :],
                     in0=kept[n]["attn", t][:],
@@ -188,13 +209,13 @@ def tile_swablock_pb_t_kernel(tc, x, o_heads, Wo, bo, gamma, beta, W1, b1, out_0
                     accum_out=row_sum[:, t : t + 1],
                 )
             minus_mean = stats.tile([P, PAIR], F32)
-            nc.scalar.mul(out=minus_mean[:], in_=row_sum[:], mul=-1.0 / D)
+            nc.scalar.mul(out=minus_mean[:, 0 : SIZES[n]], in_=row_sum[:, 0 : SIZES[n]], mul=-1.0 / D)
             kept[n]["r"] = r
             kept[n]["minus_mean"] = minus_mean
 
         def variance(n):
             sum_sq = stats.tile([P, PAIR], F32)
-            for t in range(PAIR):
+            for t in range(SIZES[n]):
                 squares = work.tile([P, D], BF16)
                 nc.scalar.activation(
                     out=squares[:],
@@ -207,17 +228,18 @@ def tile_swablock_pb_t_kernel(tc, x, o_heads, Wo, bo, gamma, beta, W1, b1, out_0
             kept[n]["sum_sq"] = sum_sq
 
         def inverse_deviation(n):
+            s = SIZES[n]
             var_eps = stats.tile([P, PAIR], F32)
             nc.scalar.activation(
-                out=var_eps[:], in_=kept[n]["sum_sq"][:], func=ACT.Identity, scale=1.0 / D, bias=EPS
+                out=var_eps[:, 0:s], in_=kept[n]["sum_sq"][:, 0:s], func=ACT.Identity, scale=1.0 / D, bias=EPS
             )
             rstd = stats.tile([P, PAIR], F32)
-            nc.gpsimd.tensor_tensor(out=rstd[:], in0=var_eps[:], in1=minus_half[:], op=ALU.pow)
+            nc.gpsimd.tensor_tensor(out=rstd[:, 0:s], in0=var_eps[:, 0:s], in1=minus_half[:, 0:s], op=ALU.pow)
             kept[n]["rstd"] = rstd
 
         def centre(n):
             centred = work.tile([P, PAIR, D], F32)
-            for t in range(PAIR):
+            for t in range(SIZES[n]):
                 nc.vector.scalar_tensor_tensor(
                     out=centred[:, t, :],
                     in0=kept[n]["r"][:, t, :],
@@ -230,7 +252,7 @@ def tile_swablock_pb_t_kernel(tc, x, o_heads, Wo, bo, gamma, beta, W1, b1, out_0
 
         def normalise(n):
             xn = stores.tile([P, PAIR, D], F32)
-            for t in range(PAIR):
+            for t in range(SIZES[n]):
                 nc.vector.scalar_tensor_tensor(
                     out=xn[:, t, :],
                     in0=kept[n]["centred"][:, t, :],
@@ -239,11 +261,11 @@ def tile_swablock_pb_t_kernel(tc, x, o_heads, Wo, bo, gamma, beta, W1, b1, out_0
                     op0=ALU.mult,
                     op1=ALU.add,
                 )
-            nc.sync.dma_start(out=xn_rounds[n], in_=xn[:])
+            nc.sync.dma_start(out=round_of(out_0, n), in_=xn[:, 0 : SIZES[n], :])
             kept[n]["xn"] = xn
 
         def transpose_xn(n):
-            for t in range(PAIR):
+            for t in range(SIZES[n]):
                 xn_t = psum_xt.tile([P, PACK, P], F32)
                 for j in range(PACK):
                     nc.tensor.transpose(xn_t[:, j, :], kept[n]["xn"][:, t, P * j : P * (j + 1)], identity[:])
@@ -251,7 +273,7 @@ def tile_swablock_pb_t_kernel(tc, x, o_heads, Wo, bo, gamma, beta, W1, b1, out_0
 
         def copy_xn_t(n):
             xn_grouped = mx.tile([P, PAIR, P, PACK], BF16, align_bytes=64)
-            for t in range(PAIR):
+            for t in range(SIZES[n]):
                 nc.scalar.copy(
                     out=xn_grouped[:, t, :, :], in_=kept[n]["xn_t", t][:].rearrange("q j r -> q r j")
                 )
@@ -261,22 +283,22 @@ def tile_swablock_pb_t_kernel(tc, x, o_heads, Wo, bo, gamma, beta, W1, b1, out_0
             xn_codes = mx.tile([P, PAIR * P], U32, align_bytes=64)
             xn_scales = mx.tile([P, PAIR * P], U8, align_bytes=64)
             nc.vector.quantize_mx(
-                out=xn_codes[:].bitcast(FP8X4),
-                scales=xn_scales[:],
-                in_=kept[n]["xn_grouped"][:].rearrange("q t r j -> q (t r j)"),
+                out=xn_codes[:, 0 : P * SIZES[n]].bitcast(FP8X4),
+                scales=xn_scales[:, 0 : P * SIZES[n]],
+                in_=kept[n]["xn_grouped"][:, 0 : SIZES[n], :, :].rearrange("q t r j -> q (t r j)"),
             )
             kept[n]["xn_codes"] = xn_codes
             kept[n]["xn_scales"] = xn_scales
 
         def mlp_matmul(n):
-            mlp_t = psum_mlp.tile([P, F_TILES, PAIR * P], F32)
+            mlp_t = psum_mlp.tile([P, F_TILES, PAIR * P], F32, tag="mlp_t")
             for c in range(F_TILES):
                 nc.tensor.matmul_mx(
-                    out=mlp_t[:, c, :],
+                    out=mlp_t[:, c, 0 : P * SIZES[n]],
                     lhsT=w1_codes[:, P * c : P * (c + 1)].bitcast(FP8X4),
                     lhsT_scale=w1_scales[:, P * c : P * (c + 1)],
-                    rhs=kept[n]["xn_codes"][:].bitcast(FP8X4),
-                    rhs_scale=kept[n]["xn_scales"][:],
+                    rhs=kept[n]["xn_codes"][:, 0 : P * SIZES[n]].bitcast(FP8X4),
+                    rhs_scale=kept[n]["xn_scales"][:, 0 : P * SIZES[n]],
                     start=True,
                     stop=True,
                 )
@@ -286,8 +308,8 @@ def tile_swablock_pb_t_kernel(tc, x, o_heads, Wo, bo, gamma, beta, W1, b1, out_0
             h_t = work.tile([P, F_TILES, PAIR * P], F32)
             for c in range(F_TILES):
                 nc.scalar.activation(
-                    out=h_t[:, c, :],
-                    in_=kept[n]["mlp_t"][:, c, :],
+                    out=h_t[:, c, 0 : P * SIZES[n]],
+                    in_=kept[n]["mlp_t"][:, c, 0 : P * SIZES[n]],
                     func=ACT.Gelu,
                     bias=b1_column[:, c : c + 1],
                     scale=1.0,
@@ -296,7 +318,7 @@ def tile_swablock_pb_t_kernel(tc, x, o_heads, Wo, bo, gamma, beta, W1, b1, out_0
 
         def transpose_h(n):
             h_psum = psum_h.tile([P, PAIR, F_TILES, P], F32)
-            for t in range(PAIR):
+            for t in range(SIZES[n]):
                 for c in range(F_TILES):
                     nc.tensor.transpose(
                         h_psum[:, t, c, :], kept[n]["h_t"][:, c, P * t : P * (t + 1)], identity[:]
@@ -305,8 +327,9 @@ def tile_swablock_pb_t_kernel(tc, x, o_heads, Wo, bo, gamma, beta, W1, b1, out_0
 
         def copy_h(n):
             h = stores.tile([P, PAIR, F], F32)
-            nc.scalar.copy(out=h[:], in_=kept[n]["h_psum"][:].rearrange("p t c f -> p t (c f)"))
-            nc.sync.dma_start(out=h_rounds[n], in_=h[:])
+            s = SIZES[n]
+            nc.scalar.copy(out=h[:, 0:s, :], in_=kept[n]["h_psum"][:, 0:s, :, :].rearrange("p t c f -> p t (c f)"))
+            nc.sync.dma_start(out=round_of(out_1, n), in_=h[:, 0:s, :])
 
         def step(work_of, n):
             if 0 <= n < ROUNDS:
@@ -314,8 +337,16 @@ def tile_swablock_pb_t_kernel(tc, x, o_heads, Wo, bo, gamma, beta, W1, b1, out_0
 
         with tc.manual_schedule():
             for turn in range(-4, ROUNDS + 5):
-                step(load, turn + 5)
+                if turn + 5 > 1:
+                    step(load_o, turn + 5)
+                    step(load_x, turn + 5)
                 step(copy_o_t, turn + 2)
+                if turn == -2:
+                    spread_bo()
+                    spread_others()
+                    quantise_wo()
+                if turn == -1:
+                    quantise_w1()
                 step(transpose_h, turn - 5)
                 step(copy_xn_t, turn - 2)
                 step(mlp_matmul, turn - 3)
@@ -327,8 +358,8 @@ def tile_swablock_pb_t_kernel(tc, x, o_heads, Wo, bo, gamma, beta, W1, b1, out_0
                 step(variance, turn)
                 step(gelu, turn - 3)
                 step(inverse_deviation, turn)
+                step(centre, turn - 1)
                 step(normalise, turn - 1)
-                step(transpose_xn, turn - 1)
                 step(transpose_o, turn + 3)
-                step(centre, turn)
+                step(transpose_xn, turn - 1)
                 step(quantise_xn, turn - 2)

@@ -22,6 +22,7 @@ ONES_COLS = 64
 SIZES = [1] + [PAIR] * (TOKENS // (PAIR * P) - 1) + [1]
 ROUNDS = len(SIZES)
 EPS = 1e-5
+WO_VECTOR = 320
 
 FLOPS = 2 * TOKENS * D * (D + F)
 
@@ -61,7 +62,7 @@ def tile_swablock_pb_t_kernel(tc, x, o_heads, Wo, bo, gamma, beta, W1, b1, out_0
             kept[n]["x_sb"] = x_sb
 
         bo_row = consts.tile([P, D], BF16)
-        nc.vector.memset(bo_row[:], 0.0)
+        nc.gpsimd.memset(bo_row[:], 0.0)
         vec_rows = consts.tile([P, 2 * D + F], BF16)
         nc.vector.memset(vec_rows[:], 0.0)
         minus_half = consts.tile([P, PAIR], F32)
@@ -74,13 +75,13 @@ def tile_swablock_pb_t_kernel(tc, x, o_heads, Wo, bo, gamma, beta, W1, b1, out_0
         nc.scalar.activation(out=gelu_warm[:], in_=minus_half[:, 0:1], func=ACT.Gelu, bias=0.0, scale=1.0)
 
         wo_rows = consts.tile([P, PACK, D], BF16)
+        nc.sync.dma_start(out=bo_row[0:1, :], in_=bo.unsqueeze(0))
+        load_o(0)
         for u in range(2):
-            nc.scalar.dma_start(
+            nc.sync.dma_start(
                 out=wo_rows[:, 2 * u : 2 * u + 2, :],
                 in_=Wo[256 * u : 256 * u + 256, :].rearrange("(q e) c -> q e c", e=2),
             )
-        load_o(0)
-        nc.sync.dma_start(out=bo_row[0:1, :], in_=bo.unsqueeze(0))
         load_x(0)
         nc.sync.dma_start(out=vec_rows[0:1, 0:D], in_=gamma.unsqueeze(0))
         nc.sync.dma_start(out=vec_rows[0:1, D : 2 * D], in_=beta.unsqueeze(0))
@@ -98,7 +99,9 @@ def tile_swablock_pb_t_kernel(tc, x, o_heads, Wo, bo, gamma, beta, W1, b1, out_0
         w1_scales = consts.tile([P, F], U8, align_bytes=64)
 
         def quantise_wo():
-            nc.vector.tensor_copy(out=wo_grouped[:], in_=wo_rows[:].rearrange("q j c -> q c j"))
+            grouped = wo_rows[:].rearrange("q j c -> q c j")
+            nc.vector.tensor_copy(out=wo_grouped[:, 0:WO_VECTOR, :], in_=grouped[:, 0:WO_VECTOR, :])
+            nc.scalar.copy(out=wo_grouped[:, WO_VECTOR:, :], in_=grouped[:, WO_VECTOR:, :])
             nc.vector.quantize_mx(
                 out=wo_codes[:].bitcast(FP8X4),
                 scales=wo_scales[:],
@@ -122,10 +125,11 @@ def tile_swablock_pb_t_kernel(tc, x, o_heads, Wo, bo, gamma, beta, W1, b1, out_0
         def spread_bo():
             bo_psum = psum_attn.tile([P, D], F32, tag="attn")
             nc.tensor.matmul(out=bo_psum[:], lhsT=ones[:], rhs=bo_row[:], start=True, stop=True)
-            for t in range(PAIR):
-                nc.scalar.copy(out=bo_all[:, t, :], in_=bo_psum[:])
+            nc.scalar.copy(out=bo_all[:, 0, :], in_=bo_psum[:])
+            return bo_psum
 
-        def spread_others():
+        def spread_others(bo_psum):
+            nc.scalar.copy(out=bo_all[:, 1, :], in_=bo_psum[:])
             for i in range(2):
                 nc.tensor.matmul(
                     out=gamma_beta[:, i, :],
@@ -208,9 +212,18 @@ def tile_swablock_pb_t_kernel(tc, x, o_heads, Wo, bo, gamma, beta, W1, b1, out_0
                     op1=ALU.add,
                     accum_out=row_sum[:, t : t + 1],
                 )
-            minus_mean = stats.tile([P, PAIR], F32)
-            nc.scalar.mul(out=minus_mean[:, 0 : SIZES[n]], in_=row_sum[:, 0 : SIZES[n]], mul=-1.0 / D)
             kept[n]["r"] = r
+            kept[n]["row_sum"] = row_sum
+
+        def negate_mean(n):
+            minus_mean = stats.tile([P, PAIR], F32)
+            nc.vector.tensor_scalar(
+                out=minus_mean[:, 0 : SIZES[n]],
+                in0=kept[n]["row_sum"][:, 0 : SIZES[n]],
+                scalar1=-1.0 / D,
+                scalar2=None,
+                op0=ALU.mult,
+            )
             kept[n]["minus_mean"] = minus_mean
 
         def variance(n):
@@ -237,25 +250,25 @@ def tile_swablock_pb_t_kernel(tc, x, o_heads, Wo, bo, gamma, beta, W1, b1, out_0
             nc.gpsimd.tensor_tensor(out=rstd[:, 0:s], in0=var_eps[:, 0:s], in1=minus_half[:, 0:s], op=ALU.pow)
             kept[n]["rstd"] = rstd
 
-        def centre(n):
-            centred = work.tile([P, PAIR, D], F32)
-            for t in range(SIZES[n]):
+        def centre(n, t):
+            if t < SIZES[n]:
+                centred = work.tile([P, D], F32, tag=f"centred{t}")
                 nc.vector.scalar_tensor_tensor(
-                    out=centred[:, t, :],
+                    out=centred[:],
                     in0=kept[n]["r"][:, t, :],
                     scalar=kept[n]["minus_mean"][:, t : t + 1],
                     in1=gamma_all,
                     op0=ALU.add,
                     op1=ALU.mult,
                 )
-            kept[n]["centred"] = centred
+                kept[n]["centred", t] = centred
 
         def normalise(n):
             xn = stores.tile([P, PAIR, D], F32)
             for t in range(SIZES[n]):
                 nc.vector.scalar_tensor_tensor(
                     out=xn[:, t, :],
-                    in0=kept[n]["centred"][:, t, :],
+                    in0=kept[n]["centred", t][:],
                     scalar=kept[n]["rstd"][:, t : t + 1],
                     in1=beta_all,
                     op0=ALU.mult,
@@ -331,34 +344,37 @@ def tile_swablock_pb_t_kernel(tc, x, o_heads, Wo, bo, gamma, beta, W1, b1, out_0
             nc.scalar.copy(out=h[:, 0:s, :], in_=kept[n]["h_psum"][:, 0:s, :, :].rearrange("p t c f -> p t (c f)"))
             nc.sync.dma_start(out=round_of(out_1, n), in_=h[:, 0:s, :])
 
-        def step(work_of, n):
+        def step(work_of, n, *tile):
             if 0 <= n < ROUNDS:
-                work_of(n)
+                work_of(n, *tile)
 
         with tc.manual_schedule():
-            for turn in range(-4, ROUNDS + 5):
+            for turn in range(-4, ROUNDS + 4):
                 if turn + 5 > 1:
                     step(load_o, turn + 5)
                     step(load_x, turn + 5)
+                if turn == -3:
+                    bo_psum = spread_bo()
                 step(copy_o_t, turn + 2)
                 if turn == -2:
-                    spread_bo()
-                    spread_others()
                     quantise_wo()
+                    spread_others(bo_psum)
                 if turn == -1:
                     quantise_w1()
-                step(transpose_h, turn - 5)
                 step(copy_xn_t, turn - 2)
                 step(mlp_matmul, turn - 3)
                 step(quantise_o, turn + 1)
                 step(add_bo, turn + 2)
                 step(residual, turn)
                 step(attn_matmul, turn + 1)
-                step(copy_h, turn - 5)
+                step(transpose_h, turn - 4)
+                step(centre, turn - 1, 0)
+                step(negate_mean, turn)
+                step(centre, turn - 1, 1)
                 step(variance, turn)
                 step(gelu, turn - 3)
                 step(inverse_deviation, turn)
-                step(centre, turn - 1)
+                step(copy_h, turn - 4)
                 step(normalise, turn - 1)
                 step(transpose_o, turn + 3)
                 step(transpose_xn, turn - 1)

@@ -116,7 +116,7 @@ def tile_swablock_pb_t_kernel(tc, x, o_heads, Wo, bo, gamma, beta, W1, b1, out_0
                 in_=w1_grouped[:].rearrange("q f j -> q (f j)"),
             )
 
-        bo_all = consts.tile([P, PAIR, D], F32)
+        bo_all = consts.tile([P, D], F32)
         gamma_beta = psum_vec.tile([P, 2, D], BF16)
         gamma_all = gamma_beta[:, 0, :]
         beta_all = gamma_beta[:, 1, :]
@@ -125,11 +125,9 @@ def tile_swablock_pb_t_kernel(tc, x, o_heads, Wo, bo, gamma, beta, W1, b1, out_0
         def spread_bo():
             bo_psum = psum_attn.tile([P, D], F32, tag="attn")
             nc.tensor.matmul(out=bo_psum[:], lhsT=ones[:], rhs=bo_row[:], start=True, stop=True)
-            nc.scalar.copy(out=bo_all[:, 0, :], in_=bo_psum[:])
-            return bo_psum
+            nc.scalar.copy(out=bo_all[:], in_=bo_psum[:])
 
-        def spread_others(bo_psum):
-            nc.scalar.copy(out=bo_all[:, 1, :], in_=bo_psum[:])
+        def spread_others():
             for i in range(2):
                 nc.tensor.matmul(
                     out=gamma_beta[:, i, :],
@@ -151,12 +149,10 @@ def tile_swablock_pb_t_kernel(tc, x, o_heads, Wo, bo, gamma, beta, W1, b1, out_0
 
 
         def add_bo(n):
-            x_bo = work.tile([P, PAIR, D], F32, bufs=4)
-            s = SIZES[n]
-            nc.gpsimd.tensor_tensor(
-                out=x_bo[:, 0:s, :], in0=kept[n]["x_sb"][:, 0:s, :], in1=bo_all[:, 0:s, :], op=ALU.add
-            )
-            kept[n]["x_bo"] = x_bo
+            for t in range(SIZES[n]):
+                x_bo = work.tile([P, D], F32, tag=f"x_bo{t}", bufs=4)
+                nc.gpsimd.tensor_tensor(out=x_bo[:], in0=kept[n]["x_sb"][:, t, :], in1=bo_all[:], op=ALU.add)
+                kept[n]["x_bo", t] = x_bo
 
         def transpose_o(n):
             o_words = kept[n]["o_sb"][:].bitcast(F32)
@@ -207,7 +203,7 @@ def tile_swablock_pb_t_kernel(tc, x, o_heads, Wo, bo, gamma, beta, W1, b1, out_0
                     out=r[:, t, :],
                     in0=kept[n]["attn", t][:],
                     scalar=1.0,
-                    in1=kept[n]["x_bo"][:, t, :],
+                    in1=kept[n]["x_bo", t][:],
                     op0=ALU.mult,
                     op1=ALU.add,
                     accum_out=row_sum[:, t : t + 1],
@@ -217,13 +213,7 @@ def tile_swablock_pb_t_kernel(tc, x, o_heads, Wo, bo, gamma, beta, W1, b1, out_0
 
         def negate_mean(n):
             minus_mean = stats.tile([P, PAIR], F32)
-            nc.vector.tensor_scalar(
-                out=minus_mean[:, 0 : SIZES[n]],
-                in0=kept[n]["row_sum"][:, 0 : SIZES[n]],
-                scalar1=-1.0 / D,
-                scalar2=None,
-                op0=ALU.mult,
-            )
+            nc.scalar.mul(out=minus_mean[:, 0 : SIZES[n]], in_=kept[n]["row_sum"][:, 0 : SIZES[n]], mul=-1.0 / D)
             kept[n]["minus_mean"] = minus_mean
 
         def variance(n):
@@ -250,8 +240,8 @@ def tile_swablock_pb_t_kernel(tc, x, o_heads, Wo, bo, gamma, beta, W1, b1, out_0
             nc.gpsimd.tensor_tensor(out=rstd[:, 0:s], in0=var_eps[:, 0:s], in1=minus_half[:, 0:s], op=ALU.pow)
             kept[n]["rstd"] = rstd
 
-        def centre(n, t):
-            if t < SIZES[n]:
+        def centre(n):
+            for t in range(SIZES[n]):
                 centred = work.tile([P, D], F32, tag=f"centred{t}")
                 nc.vector.scalar_tensor_tensor(
                     out=centred[:],
@@ -344,37 +334,36 @@ def tile_swablock_pb_t_kernel(tc, x, o_heads, Wo, bo, gamma, beta, W1, b1, out_0
             nc.scalar.copy(out=h[:, 0:s, :], in_=kept[n]["h_psum"][:, 0:s, :, :].rearrange("p t c f -> p t (c f)"))
             nc.sync.dma_start(out=round_of(out_1, n), in_=h[:, 0:s, :])
 
-        def step(work_of, n, *tile):
+        def step(work_of, n):
             if 0 <= n < ROUNDS:
-                work_of(n, *tile)
+                work_of(n)
 
         with tc.manual_schedule():
-            for turn in range(-4, ROUNDS + 4):
+            for turn in range(-4, ROUNDS + 5):
                 if turn + 5 > 1:
                     step(load_o, turn + 5)
                     step(load_x, turn + 5)
                 if turn == -3:
-                    bo_psum = spread_bo()
+                    spread_bo()
                 step(copy_o_t, turn + 2)
                 if turn == -2:
                     quantise_wo()
-                    spread_others(bo_psum)
+                    spread_others()
                 if turn == -1:
                     quantise_w1()
+                step(transpose_h, turn - 5)
                 step(copy_xn_t, turn - 2)
                 step(mlp_matmul, turn - 3)
                 step(quantise_o, turn + 1)
-                step(add_bo, turn + 2)
+                step(add_bo, turn + 1)
                 step(residual, turn)
-                step(attn_matmul, turn + 1)
-                step(transpose_h, turn - 4)
-                step(centre, turn - 1, 0)
                 step(negate_mean, turn)
-                step(centre, turn - 1, 1)
+                step(attn_matmul, turn + 1)
+                step(copy_h, turn - 5)
                 step(variance, turn)
                 step(gelu, turn - 3)
                 step(inverse_deviation, turn)
-                step(copy_h, turn - 4)
+                step(centre, turn - 1)
                 step(normalise, turn - 1)
                 step(transpose_o, turn + 3)
                 step(transpose_xn, turn - 1)

@@ -22,6 +22,7 @@ ONES_COLS = 64
 SIZES = [1] + [PAIR] * (TOKENS // (PAIR * P) - 1) + [1]
 ROUNDS = len(SIZES)
 EPS = 1e-5
+VECTOR_BO_ROUNDS = 2
 WO_VECTOR = 320
 
 FLOPS = 2 * TOKENS * D * (D + F)
@@ -108,8 +109,10 @@ def tile_swablock_pb_t_kernel(tc, x, o_heads, Wo, bo, gamma, beta, W1, b1, out_0
                 in_=wo_grouped[:].rearrange("q c j -> q (c j)"),
             )
 
-        def quantise_w1():
+        def group_w1():
             nc.scalar.copy(out=w1_grouped[:], in_=w1_rows[:].rearrange("q j f -> q f j"))
+
+        def quantise_w1():
             nc.vector.quantize_mx(
                 out=w1_codes[:].bitcast(FP8X4),
                 scales=w1_scales[:],
@@ -149,14 +152,15 @@ def tile_swablock_pb_t_kernel(tc, x, o_heads, Wo, bo, gamma, beta, W1, b1, out_0
 
 
         def add_bo(n):
+            engine = nc.vector if n < VECTOR_BO_ROUNDS else nc.gpsimd
             for t in range(SIZES[n]):
                 x_bo = work.tile([P, D], F32, tag=f"x_bo{t}", bufs=4)
-                nc.gpsimd.tensor_tensor(out=x_bo[:], in0=kept[n]["x_sb"][:, t, :], in1=bo_all[:], op=ALU.add)
+                engine.tensor_tensor(out=x_bo[:], in0=kept[n]["x_sb"][:, t, :], in1=bo_all[:], op=ALU.add)
                 kept[n]["x_bo", t] = x_bo
 
         def transpose_o(n):
             o_words = kept[n]["o_sb"][:].bitcast(F32)
-            o_t = psum_o.tile([P, PAIR, 2, P], F32)
+            o_t = psum_o.tile([P, PAIR, 2, P], F32, tag="o_t")
             for t in range(SIZES[n]):
                 for u in range(2):
                     nc.tensor.transpose(o_t[:, t, u, :], o_words[:, t, P * u : P * (u + 1)], identity[:])
@@ -294,7 +298,10 @@ def tile_swablock_pb_t_kernel(tc, x, o_heads, Wo, bo, gamma, beta, W1, b1, out_0
             kept[n]["xn_scales"] = xn_scales
 
         def mlp_matmul(n):
-            mlp_t = psum_mlp.tile([P, F_TILES, PAIR * P], F32, tag="mlp_t")
+            if n == ROUNDS - 2:
+                mlp_t = psum_attn.tile([P, F_TILES, PAIR * P], F32, tag="attn")
+            else:
+                mlp_t = psum_mlp.tile([P, F_TILES, PAIR * P], F32, tag="mlp_t")
             for c in range(F_TILES):
                 nc.tensor.matmul_mx(
                     out=mlp_t[:, c, 0 : P * SIZES[n]],
@@ -320,7 +327,12 @@ def tile_swablock_pb_t_kernel(tc, x, o_heads, Wo, bo, gamma, beta, W1, b1, out_0
             kept[n]["h_t"] = h_t
 
         def transpose_h(n):
-            h_psum = psum_h.tile([P, PAIR, F_TILES, P], F32)
+            if n == ROUNDS - 1:
+                h_psum = psum_attn.tile([P, PAIR, F_TILES, P], F32, tag="attn")
+            elif n in (ROUNDS - 2, ROUNDS - 4):
+                h_psum = psum_o.tile([P, PAIR, F_TILES, P], F32, tag="o_t")
+            else:
+                h_psum = psum_h.tile([P, PAIR, F_TILES, P], F32)
             for t in range(SIZES[n]):
                 for c in range(F_TILES):
                     nc.tensor.transpose(
@@ -331,7 +343,11 @@ def tile_swablock_pb_t_kernel(tc, x, o_heads, Wo, bo, gamma, beta, W1, b1, out_0
         def copy_h(n):
             h = stores.tile([P, PAIR, F], F32)
             s = SIZES[n]
-            nc.scalar.copy(out=h[:, 0:s, :], in_=kept[n]["h_psum"][:, 0:s, :, :].rearrange("p t c f -> p t (c f)"))
+            h_sums = kept[n]["h_psum"][:, 0:s, :, :].rearrange("p t c f -> p t (c f)")
+            if ROUNDS - 5 <= n < ROUNDS - 1:
+                nc.vector.tensor_copy(out=h[:, 0:s, :], in_=h_sums)
+            else:
+                nc.scalar.copy(out=h[:, 0:s, :], in_=h_sums)
             nc.sync.dma_start(out=round_of(out_1, n), in_=h[:, 0:s, :])
 
         def step(work_of, n):
@@ -345,26 +361,31 @@ def tile_swablock_pb_t_kernel(tc, x, o_heads, Wo, bo, gamma, beta, W1, b1, out_0
                     step(load_x, turn + 5)
                 if turn == -3:
                     spread_bo()
+                step(transpose_h, turn - 5)
+                step(copy_xn_t, turn - 2)
+                step(mlp_matmul, turn - 3)
+                step(quantise_o, turn + 1)
+                step(residual, turn)
+                step(add_bo, turn + 1)
+                step(negate_mean, turn)
+                step(attn_matmul, turn + 1)
                 step(copy_o_t, turn + 2)
                 if turn == -2:
                     quantise_wo()
                     spread_others()
                 if turn == -1:
-                    quantise_w1()
-                step(transpose_h, turn - 5)
-                step(copy_xn_t, turn - 2)
-                step(mlp_matmul, turn - 3)
-                step(quantise_o, turn + 1)
-                step(add_bo, turn + 1)
-                step(residual, turn)
-                step(negate_mean, turn)
-                step(attn_matmul, turn + 1)
-                step(copy_h, turn - 5)
+                    group_w1()
                 step(variance, turn)
-                step(gelu, turn - 3)
+                if turn < ROUNDS:
+                    step(copy_h, turn - 5)
                 step(inverse_deviation, turn)
+                step(gelu, turn - 3)
                 step(centre, turn - 1)
                 step(normalise, turn - 1)
+                if turn >= ROUNDS:
+                    step(copy_h, turn - 5)
                 step(transpose_o, turn + 3)
                 step(transpose_xn, turn - 1)
                 step(quantise_xn, turn - 2)
+                if turn == 1:
+                    quantise_w1()

@@ -23,7 +23,8 @@ SIZES = [1] + [PAIR] * (TOKENS // (PAIR * P) - 1) + [1]
 ROUNDS = len(SIZES)
 EPS = 1e-5
 VECTOR_BO_ROUNDS = 2
-WO_VECTOR = 320
+CLOCK_ROUNDS = 6
+WO_VECTOR = 384
 
 FLOPS = 2 * TOKENS * D * (D + F)
 
@@ -128,9 +129,10 @@ def tile_swablock_pb_t_kernel(tc, x, o_heads, Wo, bo, gamma, beta, W1, b1, out_0
         def spread_bo():
             bo_psum = psum_attn.tile([P, D], F32, tag="attn")
             nc.tensor.matmul(out=bo_psum[:], lhsT=ones[:], rhs=bo_row[:], start=True, stop=True)
-            nc.scalar.copy(out=bo_all[:], in_=bo_psum[:])
+            return bo_psum
 
-        def spread_others():
+        def spread_others(bo_psum):
+            nc.scalar.copy(out=bo_all[:], in_=bo_psum[:])
             for i in range(2):
                 nc.tensor.matmul(
                     out=gamma_beta[:, i, :],
@@ -274,6 +276,14 @@ def tile_swablock_pb_t_kernel(tc, x, o_heads, Wo, bo, gamma, beta, W1, b1, out_0
         def transpose_xn(n):
             for t in range(SIZES[n]):
                 xn_t = psum_xt.tile([P, PACK, P], F32)
+                if n >= ROUNDS - CLOCK_ROUNDS:
+                    nc.tensor.matmul(
+                        out=xn_t[:].rearrange("q j r -> q (j r)"),
+                        lhsT=ones[:],
+                        rhs=vec_rows[:, 0:D],
+                        start=True,
+                        stop=True,
+                    )
                 for j in range(PACK):
                     nc.tensor.transpose(xn_t[:, j, :], kept[n]["xn"][:, t, P * j : P * (j + 1)], identity[:])
                 kept[n]["xn_t", t] = xn_t
@@ -360,7 +370,9 @@ def tile_swablock_pb_t_kernel(tc, x, o_heads, Wo, bo, gamma, beta, W1, b1, out_0
                     step(load_o, turn + 5)
                     step(load_x, turn + 5)
                 if turn == -3:
-                    spread_bo()
+                    bo_psum = spread_bo()
+                if turn == -2:
+                    quantise_wo()
                 step(transpose_h, turn - 5)
                 step(copy_xn_t, turn - 2)
                 step(mlp_matmul, turn - 3)
@@ -371,8 +383,7 @@ def tile_swablock_pb_t_kernel(tc, x, o_heads, Wo, bo, gamma, beta, W1, b1, out_0
                 step(attn_matmul, turn + 1)
                 step(copy_o_t, turn + 2)
                 if turn == -2:
-                    quantise_wo()
-                    spread_others()
+                    spread_others(bo_psum)
                 if turn == -1:
                     group_w1()
                 step(variance, turn)

from contextlib import ExitStack

import concourse.mybir as mybir
from concourse.masks import make_identity

F32 = mybir.dt.float32
BF16 = mybir.dt.bfloat16
U32 = mybir.dt.uint32
U8 = mybir.dt.uint8
FP8X4 = mybir.dt.float8_e4m3fn_x4
ALU = mybir.AluOpType
ACT = mybir.ActivationFunctionType

P = 128
PACK = 4
D = 512
F = 256
TOKENS = 4 * 1536
F_TILES = F // P
PAIR = 2
ONES_COLS = 64
SIZES = [1] + [PAIR] * (TOKENS // (PAIR * P) - 1) + [1]
ROUNDS = len(SIZES)
EPS = 1e-5
VECTOR_BO_ROUNDS = 2
CLOCK_ROUNDS = 6
WO_VECTOR = 384

FLOPS = 2 * TOKENS * D * (D + F)


def tile_swablock_pb_t_kernel(tc, x, o_heads, Wo, bo, gamma, beta, W1, b1, out_0, out_1):
    nc = tc.nc

    def round_of(tensor, n):
        first = P * sum(SIZES[:n])
        rows = tensor.flatten_outer_dims()[first : first + P * SIZES[n], :]
        return rows.rearrange("(p t) d -> p t d", p=P, t=SIZES[n])

    with ExitStack() as ctx:
        consts = ctx.enter_context(tc.tile_pool(name="consts", bufs=1))
        loads = ctx.enter_context(tc.tile_pool(name="loads", bufs=5))
        work = ctx.enter_context(tc.tile_pool(name="work", bufs=3))
        mx = ctx.enter_context(tc.tile_pool(name="mx", bufs=2))
        stats = ctx.enter_context(tc.tile_pool(name="stats", bufs=4))
        stores = ctx.enter_context(tc.tile_pool(name="stores", bufs=4))
        psum_vec = ctx.enter_context(tc.psum_pool(name="psum_vec", bufs=1))
        psum_o = ctx.enter_context(tc.psum_pool(name="psum_o", bufs=1))
        psum_h = ctx.enter_context(tc.psum_pool(name="psum_h", bufs=1))
        psum_attn = ctx.enter_context(tc.psum_pool(name="psum_attn", bufs=2))
        psum_xt = ctx.enter_context(tc.psum_pool(name="psum_xt", bufs=2))
        psum_mlp = ctx.enter_context(tc.psum_pool(name="psum_mlp", bufs=1))

        kept = [{} for n in range(ROUNDS)]

        def load_o(n):
            o_sb = loads.tile([P, PAIR, D], BF16)
            nc.sync.dma_start(out=o_sb[:, 0 : SIZES[n], :], in_=round_of(o_heads, n))
            kept[n]["o_sb"] = o_sb

        def load_x(n):
            x_sb = loads.tile([P, PAIR, D], BF16)
            nc.sync.dma_start(out=x_sb[:, 0 : SIZES[n], :], in_=round_of(x, n))
            kept[n]["x_sb"] = x_sb

        bo_row = consts.tile([P, D], BF16)
        nc.gpsimd.memset(bo_row[:], 0.0)
        vec_rows = consts.tile([P, 2 * D + F], BF16)
        nc.vector.memset(vec_rows[:], 0.0)
        minus_half = consts.tile([P, PAIR], F32)
        nc.vector.memset(minus_half[:], -0.5)
        ones = consts.tile([P, P], BF16)
        nc.vector.memset(ones[:], 1.0)
        identity = consts.tile([P, P], F32)
        make_identity(nc, identity[:])
        gelu_warm = consts.tile([P, 1], F32)
        nc.scalar.activation(out=gelu_warm[:], in_=minus_half[:, 0:1], func=ACT.Gelu, bias=0.0, scale=1.0)

        wo_rows = consts.tile([P, PACK, D], BF16)
        nc.sync.dma_start(out=bo_row[0:1, :], in_=bo.unsqueeze(0))
        load_o(0)
        for u in range(2):
            nc.sync.dma_start(
                out=wo_rows[:, 2 * u : 2 * u + 2, :],
                in_=Wo[256 * u : 256 * u + 256, :].rearrange("(q e) c -> q e c", e=2),
            )
        load_x(0)
        nc.sync.dma_start(out=vec_rows[0:1, 0:D], in_=gamma.unsqueeze(0))
        nc.sync.dma_start(out=vec_rows[0:1, D : 2 * D], in_=beta.unsqueeze(0))
        nc.sync.dma_start(out=vec_rows[0:1, 2 * D : 2 * D + F], in_=b1.unsqueeze(0))
        load_o(1)
        load_x(1)
        w1_rows = consts.tile([P, PACK, F], BF16)
        nc.sync.dma_start(out=w1_rows[:], in_=W1.rearrange("(j q) f -> q j f", q=P))

        wo_grouped = consts.tile([P, D, PACK], BF16, align_bytes=64)
        wo_codes = consts.tile([P, D], U32, align_bytes=64)
        wo_scales = consts.tile([P, D], U8, align_bytes=64)
        w1_grouped = consts.tile([P, F, PACK], BF16, align_bytes=64)
        w1_codes = consts.tile([P, F], U32, align_bytes=64)
        w1_scales = consts.tile([P, F], U8, align_bytes=64)

        def quantise_wo():
            grouped = wo_rows[:].rearrange("q j c -> q c j")
            nc.vector.tensor_copy(out=wo_grouped[:, 0:WO_VECTOR, :], in_=grouped[:, 0:WO_VECTOR, :])
            nc.scalar.copy(out=wo_grouped[:, WO_VECTOR:, :], in_=grouped[:, WO_VECTOR:, :])
            nc.vector.quantize_mx(
                out=wo_codes[:].bitcast(FP8X4),
                scales=wo_scales[:],
                in_=wo_grouped[:].rearrange("q c j -> q (c j)"),
            )

        def group_w1():
            nc.scalar.copy(out=w1_grouped[:], in_=w1_rows[:].rearrange("q j f -> q f j"))

        def quantise_w1():
            nc.vector.quantize_mx(
                out=w1_codes[:].bitcast(FP8X4),
                scales=w1_scales[:],
                in_=w1_grouped[:].rearrange("q f j -> q (f j)"),
            )

        bo_all = consts.tile([P, D], F32)
        gamma_beta = psum_vec.tile([P, 2, D], BF16)
        gamma_all = gamma_beta[:, 0, :]
        beta_all = gamma_beta[:, 1, :]
        b1_column = consts.tile([P, F_TILES], F32)

        def spread_bo():
            bo_psum = psum_attn.tile([P, D], F32, tag="attn")
            nc.tensor.matmul(out=bo_psum[:], lhsT=ones[:], rhs=bo_row[:], start=True, stop=True)
            return bo_psum

        def spread_others(bo_psum):
            nc.scalar.copy(out=bo_all[:], in_=bo_psum[:])
            for i in range(2):
                nc.tensor.matmul(
                    out=gamma_beta[:, i, :],
                    lhsT=ones[:],
                    rhs=vec_rows[:, i * D : (i + 1) * D],
                    start=True,
                    stop=True,
                )
            b1_psum = psum_mlp.tile([P, F_TILES, PAIR * P], F32, tag="mlp_t")
            for c in range(F_TILES):
                nc.tensor.matmul(
                    out=b1_psum[:, c, 0:ONES_COLS],
                    lhsT=vec_rows[:, 2 * D + P * c : 2 * D + P * (c + 1)],
                    rhs=ones[:, 0:ONES_COLS],
                    start=True,
                    stop=True,
                )
            nc.scalar.copy(out=b1_column[:], in_=b1_psum[:, :, 0])


        def add_bo(n):
            engine = nc.vector if n < VECTOR_BO_ROUNDS else nc.gpsimd
            for t in range(SIZES[n]):
                x_bo = work.tile([P, D], F32, tag=f"x_bo{t}", bufs=4)
                engine.tensor_tensor(out=x_bo[:], in0=kept[n]["x_sb"][:, t, :], in1=bo_all[:], op=ALU.add)
                kept[n]["x_bo", t] = x_bo

        def transpose_o(n):
            o_words = kept[n]["o_sb"][:].bitcast(F32)
            o_t = psum_o.tile([P, PAIR, 2, P], F32, tag="o_t")
            for t in range(SIZES[n]):
                for u in range(2):
                    nc.tensor.transpose(o_t[:, t, u, :], o_words[:, t, P * u : P * (u + 1)], identity[:])
            kept[n]["o_t"] = o_t

        def copy_o_t(n):
            o_grouped = mx.tile([P, PAIR, P, PACK], BF16, align_bytes=64)
            nc.scalar.copy(
                out=o_grouped[:, 0 : SIZES[n], :, :].bitcast(F32),
                in_=kept[n]["o_t"][:, 0 : SIZES[n], :, :].rearrange("q t u r -> q t r u"),
            )
            kept[n]["o_grouped"] = o_grouped

        def quantise_o(n):
            o_codes = mx.tile([P, PAIR * P], U32, align_bytes=64)
            o_scales = mx.tile([P, PAIR * P], U8, align_bytes=64)
            nc.vector.quantize_mx(
                out=o_codes[:, 0 : P * SIZES[n]].bitcast(FP8X4),
                scales=o_scales[:, 0 : P * SIZES[n]],
                in_=kept[n]["o_grouped"][:, 0 : SIZES[n], :, :].rearrange("q t r j -> q (t r j)"),
            )
            kept[n]["o_codes"] = o_codes
            kept[n]["o_scales"] = o_scales

        def attn_matmul(n):
            for t in range(SIZES[n]):
                attn = psum_attn.tile([P, D], F32, tag="attn")
                nc.tensor.matmul_mx(
                    out=attn[:],
                    lhsT=kept[n]["o_codes"][:, P * t : P * (t + 1)].bitcast(FP8X4),
                    lhsT_scale=kept[n]["o_scales"][:, P * t : P * (t + 1)],
                    rhs=wo_codes[:].bitcast(FP8X4),
                    rhs_scale=wo_scales[:],
                    start=True,
                    stop=True,
                )
                kept[n]["attn", t] = attn

        def residual(n):
            r = work.tile([P, PAIR, D], F32)
            row_sum = stats.tile([P, PAIR], F32)
            for t in range(SIZES[n]):
                nc.vector.scalar_tensor_tensor(
                    out=r[:, t, :],
                    in0=kept[n]["attn", t][:],
                    scalar=1.0,
                    in1=kept[n]["x_bo", t][:],
                    op0=ALU.mult,
                    op1=ALU.add,
                    accum_out=row_sum[:, t : t + 1],
                )
            kept[n]["r"] = r
            kept[n]["row_sum"] = row_sum

        def negate_mean(n):
            minus_mean = stats.tile([P, PAIR], F32)
            nc.scalar.mul(out=minus_mean[:, 0 : SIZES[n]], in_=kept[n]["row_sum"][:, 0 : SIZES[n]], mul=-1.0 / D)
            kept[n]["minus_mean"] = minus_mean

        def variance(n):
            sum_sq = stats.tile([P, PAIR], F32)
            for t in range(SIZES[n]):
                squares = work.tile([P, D], BF16)
                nc.scalar.activation(
                    out=squares[:],
                    in_=kept[n]["r"][:, t, :],
                    func=ACT.Square,
                    bias=kept[n]["minus_mean"][:, t : t + 1],
                    scale=1.0,
                    accum_out=sum_sq[:, t : t + 1],
                )
            kept[n]["sum_sq"] = sum_sq

        def inverse_deviation(n):
            s = SIZES[n]
            var_eps = stats.tile([P, PAIR], F32)
            nc.scalar.activation(
                out=var_eps[:, 0:s], in_=kept[n]["sum_sq"][:, 0:s], func=ACT.Identity, scale=1.0 / D, bias=EPS
            )
            rstd = stats.tile([P, PAIR], F32)
            nc.gpsimd.tensor_tensor(out=rstd[:, 0:s], in0=var_eps[:, 0:s], in1=minus_half[:, 0:s], op=ALU.pow)
            kept[n]["rstd"] = rstd

        def centre(n):
            for t in range(SIZES[n]):
                centred = work.tile([P, D], F32, tag=f"centred{t}")
                nc.vector.scalar_tensor_tensor(
                    out=centred[:],
                    in0=kept[n]["r"][:, t, :],
                    scalar=kept[n]["minus_mean"][:, t : t + 1],
                    in1=gamma_all,
                    op0=ALU.add,
                    op1=ALU.mult,
                )
                kept[n]["centred", t] = centred

        def normalise(n):
            xn = stores.tile([P, PAIR, D], F32)
            for t in range(SIZES[n]):
                nc.vector.scalar_tensor_tensor(
                    out=xn[:, t, :],
                    in0=kept[n]["centred", t][:],
                    scalar=kept[n]["rstd"][:, t : t + 1],
                    in1=beta_all,
                    op0=ALU.mult,
                    op1=ALU.add,
                )
            nc.sync.dma_start(out=round_of(out_0, n), in_=xn[:, 0 : SIZES[n], :])
            kept[n]["xn"] = xn

        def transpose_xn(n):
            for t in range(SIZES[n]):
                xn_t = psum_xt.tile([P, PACK, P], F32)
                if n >= ROUNDS - CLOCK_ROUNDS:
                    nc.tensor.matmul(
                        out=xn_t[:].rearrange("q j r -> q (j r)"),
                        lhsT=ones[:],
                        rhs=vec_rows[:, 0:D],
                        start=True,
                        stop=True,
                    )
                for j in range(PACK):
                    nc.tensor.transpose(xn_t[:, j, :], kept[n]["xn"][:, t, P * j : P * (j + 1)], identity[:])
                kept[n]["xn_t", t] = xn_t

        def copy_xn_t(n):
            xn_grouped = mx.tile([P, PAIR, P, PACK], BF16, align_bytes=64)
            for t in range(SIZES[n]):
                nc.scalar.copy(
                    out=xn_grouped[:, t, :, :], in_=kept[n]["xn_t", t][:].rearrange("q j r -> q r j")
                )
            kept[n]["xn_grouped"] = xn_grouped

        def quantise_xn(n):
            xn_codes = mx.tile([P, PAIR * P], U32, align_bytes=64)
            xn_scales = mx.tile([P, PAIR * P], U8, align_bytes=64)
            nc.vector.quantize_mx(
                out=xn_codes[:, 0 : P * SIZES[n]].bitcast(FP8X4),
                scales=xn_scales[:, 0 : P * SIZES[n]],
                in_=kept[n]["xn_grouped"][:, 0 : SIZES[n], :, :].rearrange("q t r j -> q (t r j)"),
            )
            kept[n]["xn_codes"] = xn_codes
            kept[n]["xn_scales"] = xn_scales

        def mlp_matmul(n):
            if n == ROUNDS - 2:
                mlp_t = psum_attn.tile([P, F_TILES, PAIR * P], F32, tag="attn")
            else:
                mlp_t = psum_mlp.tile([P, F_TILES, PAIR * P], F32, tag="mlp_t")
            for c in range(F_TILES):
                nc.tensor.matmul_mx(
                    out=mlp_t[:, c, 0 : P * SIZES[n]],
                    lhsT=w1_codes[:, P * c : P * (c + 1)].bitcast(FP8X4),
                    lhsT_scale=w1_scales[:, P * c : P * (c + 1)],
                    rhs=kept[n]["xn_codes"][:, 0 : P * SIZES[n]].bitcast(FP8X4),
                    rhs_scale=kept[n]["xn_scales"][:, 0 : P * SIZES[n]],
                    start=True,
                    stop=True,
                )
            kept[n]["mlp_t"] = mlp_t

        def gelu(n):
            h_t = work.tile([P, F_TILES, PAIR * P], F32)
            for c in range(F_TILES):
                nc.scalar.activation(
                    out=h_t[:, c, 0 : P * SIZES[n]],
                    in_=kept[n]["mlp_t"][:, c, 0 : P * SIZES[n]],
                    func=ACT.Gelu,
                    bias=b1_column[:, c : c + 1],
                    scale=1.0,
                )
            kept[n]["h_t"] = h_t

        def transpose_h(n):
            if n == ROUNDS - 1:
                h_psum = psum_attn.tile([P, PAIR, F_TILES, P], F32, tag="attn")
            elif n in (ROUNDS - 2, ROUNDS - 4):
                h_psum = psum_o.tile([P, PAIR, F_TILES, P], F32, tag="o_t")
            else:
                h_psum = psum_h.tile([P, PAIR, F_TILES, P], F32)
            for t in range(SIZES[n]):
                for c in range(F_TILES):
                    nc.tensor.transpose(
                        h_psum[:, t, c, :], kept[n]["h_t"][:, c, P * t : P * (t + 1)], identity[:]
                    )
            kept[n]["h_psum"] = h_psum

        def copy_h(n):
            h = stores.tile([P, PAIR, F], F32)
            s = SIZES[n]
            h_sums = kept[n]["h_psum"][:, 0:s, :, :].rearrange("p t c f -> p t (c f)")
            if ROUNDS - 5 <= n < ROUNDS - 1:
                nc.vector.tensor_copy(out=h[:, 0:s, :], in_=h_sums)
            else:
                nc.scalar.copy(out=h[:, 0:s, :], in_=h_sums)
            nc.sync.dma_start(out=round_of(out_1, n), in_=h[:, 0:s, :])

        def step(work_of, n):
            if 0 <= n < ROUNDS:
                work_of(n)

        with tc.manual_schedule():
            for turn in range(-4, ROUNDS + 5):
                if turn + 5 > 1:
                    step(load_o, turn + 5)
                    step(load_x, turn + 5)
                if turn == -3:
                    bo_psum = spread_bo()
                if turn == -2:
                    quantise_wo()
                step(transpose_h, turn - 5)
                step(copy_xn_t, turn - 2)
                step(mlp_matmul, turn - 3)
                step(quantise_o, turn + 1)
                step(residual, turn)
                step(add_bo, turn + 1)
                step(negate_mean, turn)
                step(attn_matmul, turn + 1)
                step(copy_o_t, turn + 2)
                if turn == -2:
                    spread_others(bo_psum)
                if turn == -1:
                    group_w1()
                step(variance, turn)
                if turn < ROUNDS:
                    step(copy_h, turn - 5)
                step(inverse_deviation, turn)
                step(gelu, turn - 3)
                step(centre, turn - 1)
                step(normalise, turn - 1)
                if turn >= ROUNDS:
                    step(copy_h, turn - 5)
                step(transpose_o, turn + 3)
                step(transpose_xn, turn - 1)
                step(quantise_xn, turn - 2)
                if turn == 1:
                    quantise_w1()
